import numpy as np
import ml_dtypes


def mxq(x, axis, fmt="e4m3"):
    dtype, down = {"e4m3": (ml_dtypes.float8_e4m3fn, 7), "e5m2": (ml_dtypes.float8_e5m2, 14)}[fmt]
    v = np.moveaxis(np.asarray(x, np.float32).astype(ml_dtypes.bfloat16).astype(np.float64), axis, -1)
    blocks = v.reshape(v.shape[:-1] + (-1, 32))
    amax = np.abs(blocks).max(-1, keepdims=True)
    byte = np.maximum(np.where(amax > 0, np.frexp(amax)[1] - 1 + 127, 0) - down, 1)
    scale = np.exp2(byte - 127.0)
    codes = (blocks / scale).astype(np.float32).astype(dtype).astype(np.float64)
    return np.moveaxis((codes * scale).reshape(v.shape), -1, axis)


WIDE = False


def mx_kscale(k):
    if not WIDE:
        return np.ones(k)
    levels = np.array([10, -10, 5, -5, 0])
    a = np.random.permutation(np.resize(levels, k // 512 * 4)).reshape(k // 512, 4)
    idx = np.arange(k)
    return np.exp2(a[idx // 512, idx % 128 // 32])


BF16 = ml_dtypes.bfloat16


def bf(x):
    return np.asarray(x, np.float32).astype(BF16)


def f64(x):
    return np.asarray(x).astype(np.float64)


B, C, H, W = 4, 512, 32, 32
C2 = 2 * C
N = H * W


def sigmoid(v):
    return 1.0 / (1.0 + np.exp(-v))


def setup_inputs():
    s = mx_kscale(C2)
    t = mx_kscale(C)
    return {"hsi": bf(np.random.standard_normal((B, C, H, W)) * s[:C][None, :, None, None]),
            "msi": bf(np.random.standard_normal((B, C, H, W)) * s[C:][None, :, None, None]),
            "att1": bf(np.random.standard_normal((B, C, H, W)) * 0.5 * t[None, :, None, None]),
            "att2": bf(np.random.standard_normal((B, C, H, W)) * 0.5 * t[None, :, None, None]),
            "wg": bf(np.random.standard_normal((C, C2)) / np.sqrt(C2) / s[None, :]),
            "bg": bf(np.random.standard_normal(C) * 0.2),
            "wp": bf(np.random.standard_normal((C, C)) * 2.0 / np.sqrt(C) / t[None, :]),
            "bp": bf(np.random.standard_normal(C) * 0.1)}


def reference(hsi, msi, att1, att2, wg, bg, wp, bp):
    x = np.concatenate([f64(hsi), f64(msi)], axis=1).reshape(B, C2, N)
    g = sigmoid((mxq(f64(wg), 1, "e4m3") @ mxq(x, 1, "e4m3")) + f64(bg)[None, :, None])
    fused = g * f64(att1).reshape(B, C, N) + (1.0 - g) * f64(att2).reshape(B, C, N)
    y = (mxq(f64(wp), 1, "e4m3") @ mxq(fused, 1, "e4m3")) + f64(bp)[None, :, None]
    return y.reshape(B, C, H, W)

@@ -1,0 +1,170 @@
+from contextlib import ExitStack
+
+import concourse.mybir as mybir
+from concourse.masks import make_identity
+
+F32 = mybir.dt.float32
+BF16 = mybir.dt.bfloat16
+U32 = mybir.dt.uint32
+U8 = mybir.dt.uint8
+FP8X4 = mybir.dt.float8_e4m3fn_x4
+ACT = mybir.ActivationFunctionType
+ALU = mybir.AluOpType
+
+P = 128
+B = 4
+C = 512
+NPIX = 1024
+T = 4
+CH = 512
+NCHUNK = NPIX // CH
+
+FLOPS = 2 * B * NPIX * (2 * C * C + C * C)
+
+
+def tile_crossattentionfusion_pa_t_kernel(tc, hsi, msi, att1, att2, wg, bg, wp, bp, out):
+    nc = tc.nc
+    with ExitStack() as ctx:
+        const = ctx.enter_context(tc.tile_pool(name="const", bufs=1))
+        xin = ctx.enter_context(tc.tile_pool(name="xin", bufs=2))
+        work = ctx.enter_context(tc.tile_pool(name="work", bufs=3))
+        work2 = ctx.enter_context(tc.tile_pool(name="work2", bufs=2))
+        psum = ctx.enter_context(tc.psum_pool(name="psum", bufs=3))
+
+        bg_raw = const.tile([P, T], BF16)
+        bp_raw = const.tile([P, T], BF16)
+        nc.scalar.dma_start(out=bg_raw[:], in_=bg.rearrange("(p t) -> p t", t=T))
+        nc.scalar.dma_start(out=bp_raw[:], in_=bp.rearrange("(p t) -> p t", t=T))
+        warm = const.tile([P, 1], F32)
+        nc.vector.memset(warm[:], 0.0)
+        warm2 = const.tile([P, 1], F32)
+        nc.scalar.activation(out=warm2[:], in_=warm[:], func=ACT.Sigmoid)
+        ident = const.tile([P, P], F32)
+        make_identity(nc, ident[:])
+        bgf = const.tile([P, T], F32)
+        bpf = const.tile([P, T], F32)
+        nc.vector.tensor_copy(out=bgf[:], in_=bg_raw[:])
+        nc.vector.tensor_copy(out=bpf[:], in_=bp_raw[:])
+
+        wg_raw = const.tile([P, T * 2 * C], BF16)
+        wp_raw = const.tile([P, T * C], BF16)
+        raws = {}
+
+        def load_batch(b):
+            for name, src in (("hsi", hsi), ("msi", msi), ("a1", att1), ("a2", att2)):
+                t_in = xin.tile([P, T * NPIX], BF16, tag=name, name="in_%s_%d" % (name, b))
+                nc.sync.dma_start(out=t_in[:], in_=src[b].rearrange("(p t) h w -> p (t h w)", t=T))
+                raws[(name, b)] = t_in
+
+        nc.sync.dma_start(out=wg_raw[:], in_=wg.rearrange("(m t) k -> m (t k)", t=T))
+        load_batch(0)
+        nc.sync.dma_start(out=wp_raw[:], in_=wp.rearrange("(m t) k -> m (t k)", t=T))
+
+        def prepare_weight(raw, passes, label):
+            combos = T * passes
+            words = raw[:].bitcast(F32).rearrange(
+                "m (t c p u) -> m t c p u", t=T, c=passes, p=P, u=2
+            )
+            grouped = const.tile([P, combos * P * 4], BF16, align_bytes=64, name=label + "_grouped")
+            gwords = grouped[:].bitcast(F32).rearrange("p (k m u) -> p k m u", k=combos, m=P, u=2)
+            codes = const.tile([P, combos * P], U32, align_bytes=64, name=label + "_codes")
+            scales = const.tile([P, combos * P], U8, align_bytes=64, name=label + "_scales")
+            for bank in range(combos // 2):
+                tp = psum.tile([P, 4, P], F32, tag="tp", bufs=2, name="%s_tp%d" % (label, bank))
+                for kk in range(2):
+                    k = 2 * bank + kk
+                    for u in range(2):
+                        nc.tensor.transpose(
+                            out=tp[:, 2 * kk + u, :],
+                            in_=words[:, k // passes, k % passes, :, u],
+                            identity=ident[:],
+                        )
+                src = tp[:].rearrange("p (k u) m -> p k m u", k=2, u=2)
+                dst = gwords[:, 2 * bank : 2 * bank + 2, :, :]
+                if bank % 2 == 0:
+                    nc.vector.tensor_copy(out=dst, in_=src)
+                else:
+                    nc.scalar.copy(out=dst, in_=src)
+            for half in range(combos // 4):
+                nc.vector.quantize_mx(
+                    out=codes[:, half * 512 : (half + 1) * 512].bitcast(FP8X4),
+                    scales=scales[:, half * 512 : (half + 1) * 512],
+                    in_=grouped[:, half * 2048 : (half + 1) * 2048],
+                )
+            return codes, scales
+
+        wgc, wgs = prepare_weight(wg_raw, 2, "wg")
+        wpc, wps = prepare_weight(wp_raw, 1, "wp")
+
+        for b in range(B):
+            if b + 1 < B:
+                load_batch(b + 1)
+            out_b = out[b].rearrange("(p t) h w -> p t (h w)", t=T)
+            for h in range(NCHUNK):
+                cols = slice(h * CH, (h + 1) * CH)
+
+                def plane_view(name):
+                    return raws[(name, b)][:].rearrange("p (t n) -> p t n", t=T)[:, :, cols]
+
+                xg = work.tile([P, 2, CH * T], BF16, align_bytes=64)
+                for s, name in enumerate(("hsi", "msi")):
+                    nc.scalar.copy(
+                        out=xg[:, s, :].rearrange("p (c i j) -> p c j i", i=4, j=T),
+                        in_=plane_view(name).rearrange("p j (c i) -> p c j i", i=4),
+                    )
+                xc = work.tile([P, 2, CH], U32, align_bytes=64)
+                xs = work.tile([P, 2, CH], U8, align_bytes=64)
+                nc.vector.quantize_mx(
+                    out=xc[:].rearrange("p s w -> p (s w)").bitcast(FP8X4),
+                    scales=xs[:].rearrange("p s w -> p (s w)"),
+                    in_=xg[:].rearrange("p s w -> p (s w)"),
+                )
+                d = work.tile([P, T, CH], F32)
+                nc.vector.tensor_tensor(out=d[:], in0=plane_view("a1"), in1=plane_view("a2"), op=ALU.subtract)
+
+                g = work2.tile([P, T, CH], F32)
+                for t in range(T):
+                    acc = psum.tile([P, CH], F32, tag="s1")
+                    for s in range(2):
+                        k = 2 * t + s
+                        nc.tensor.matmul_mx(
+                            out=acc[:],
+                            lhsT=wgc[:, k * P : (k + 1) * P].bitcast(FP8X4),
+                            lhsT_scale=wgs[:, k * P : (k + 1) * P],
+                            rhs=xc[:, s, :].bitcast(FP8X4),
+                            rhs_scale=xs[:, s, :],
+                            start=(s == 0),
+                            stop=(s == 1),
+                        )
+                    nc.scalar.activation(
+                        out=g[:, t, :], in_=acc[:], func=ACT.Sigmoid, bias=bgf[:, t : t + 1], scale=1.0
+                    )
+
+                nc.vector.tensor_tensor(out=d[:], in0=g[:], in1=d[:], op=ALU.mult)
+                fg = work2.tile([P, CH * T], BF16, align_bytes=64)
+                nc.vector.tensor_tensor(
+                    out=fg[:].rearrange("p (c i t) -> p c t i", i=4, t=T),
+                    in0=d[:].rearrange("p t (c i) -> p c t i", i=4),
+                    in1=plane_view("a2").rearrange("p t (c i) -> p c t i", i=4),
+                    op=ALU.add,
+                )
+                fc = work2.tile([P, CH], U32, align_bytes=64)
+                fs = work2.tile([P, CH], U8, align_bytes=64)
+                nc.vector.quantize_mx(out=fc[:].bitcast(FP8X4), scales=fs[:], in_=fg[:])
+
+                y = work.tile([P, T, CH], F32)
+                for t in range(T):
+                    acc2 = psum.tile([P, CH], F32, tag="s2")
+                    nc.tensor.matmul_mx(
+                        out=acc2[:],
+                        lhsT=wpc[:, t * P : (t + 1) * P].bitcast(FP8X4),
+                        lhsT_scale=wps[:, t * P : (t + 1) * P],
+                        rhs=fc[:].bitcast(FP8X4),
+                        rhs_scale=fs[:],
+                        start=True,
+                        stop=True,
+                    )
+                    nc.scalar.activation(
+                        out=y[:, t, :], in_=acc2[:], func=ACT.Identity, bias=bpf[:, t : t + 1], scale=1.0
+                    )
+                nc.scalar.dma_start(out=out_b[:, :, cols], in_=y[:])

@@ -17,74 +17,215 @@ C = 512
 NPIX = 1024
 T = 4
 CH = 512
-NCHUNK = NPIX // CH
+PER_B = NPIX // CH
+NCH = B * PER_B
+VS = 256
+TPE = 2
 
 FLOPS = 2 * B * NPIX * (2 * C * C + C * C)
 
 
 def tile_crossattentionfusion_pa_t_kernel(tc, hsi, msi, att1, att2, wg, bg, wp, bp, out):
     nc = tc.nc
+    sources = {"hsi": hsi, "msi": msi, "a1": att1, "a2": att2}
     with ExitStack() as ctx:
+        ctx.enter_context(tc.manual_schedule())
         const = ctx.enter_context(tc.tile_pool(name="const", bufs=1))
         xin = ctx.enter_context(tc.tile_pool(name="xin", bufs=2))
-        work = ctx.enter_context(tc.tile_pool(name="work", bufs=3))
-        work2 = ctx.enter_context(tc.tile_pool(name="work2", bufs=2))
-        psum = ctx.enter_context(tc.psum_pool(name="psum", bufs=3))
+        work = ctx.enter_context(tc.tile_pool(name="work", bufs=2))
+        psum = ctx.enter_context(tc.psum_pool(name="psum", bufs=2))
 
-        bg_raw = const.tile([P, T], BF16)
-        bp_raw = const.tile([P, T], BF16)
-        nc.scalar.dma_start(out=bg_raw[:], in_=bg.rearrange("(p t) -> p t", t=T))
-        nc.scalar.dma_start(out=bp_raw[:], in_=bp.rearrange("(p t) -> p t", t=T))
-        warm = const.tile([P, 1], F32)
-        nc.vector.memset(warm[:], 0.0)
-        warm2 = const.tile([P, 1], F32)
-        nc.scalar.activation(out=warm2[:], in_=warm[:], func=ACT.Sigmoid)
-        ident = const.tile([P, P], F32)
-        make_identity(nc, ident[:])
-        bgf = const.tile([P, T], F32)
-        bpf = const.tile([P, T], F32)
-        nc.vector.tensor_copy(out=bgf[:], in_=bg_raw[:])
-        nc.vector.tensor_copy(out=bpf[:], in_=bp_raw[:])
+        raw, xg, xc, xs, gate, mix, dps = {}, {}, {}, {}, {}, {}, {}
+        acc1, acc2, fc, fs, fg, y = {}, {}, {}, {}, {}, {}
 
-        wg_raw = const.tile([P, T * 2 * C], BF16)
-        wp_raw = const.tile([P, T * C], BF16)
-        raws = {}
+        def live(i):
+            return 0 <= i < NCH
 
-        def load_batch(b):
-            for name, src in (("hsi", hsi), ("msi", msi), ("a1", att1), ("a2", att2)):
-                t_in = xin.tile([P, T * NPIX], BF16, tag=name, name="in_%s_%d" % (name, b))
-                nc.sync.dma_start(out=t_in[:], in_=src[b].rearrange("(p t) h w -> p (t h w)", t=T))
-                raws[(name, b)] = t_in
-
-        nc.sync.dma_start(out=wg_raw[:], in_=wg.rearrange("(m t) k -> m (t k)", t=T))
-        load_batch(0)
-        nc.sync.dma_start(out=wp_raw[:], in_=wp.rearrange("(m t) k -> m (t k)", t=T))
-
-        def prepare_weight(raw, passes, label):
-            combos = T * passes
-            words = raw[:].bitcast(F32).rearrange(
-                "m (t c p u) -> m t c p u", t=T, c=passes, p=P, u=2
+        def load(name, b, lo, hi):
+            if (name, b) not in raw:
+                raw[(name, b)] = xin.tile([P, T * NPIX], BF16, tag=name, name="%s%d" % (name, b))
+            nc.sync.dma_start(
+                out=raw[(name, b)][:].rearrange("p (t n) -> p t n", t=T)[:, :, lo:hi],
+                in_=sources[name][b].rearrange("(p t) h w -> p t (h w)", t=T)[:, :, lo:hi],
             )
+
+        def planes(name, i):
+            lo = (i % PER_B) * CH
+            return raw[(name, i // PER_B)][:].rearrange("p (t n) -> p t n", t=T)[:, :, lo : lo + CH]
+
+        def regroup_part(i, copy, s, name, lo, hi):
+            copy(
+                out=xg[i][:, s, lo * T : hi * T].rearrange("p (c i j) -> p c j i", i=4, j=T),
+                in_=planes(name, i)[:, :, lo:hi].rearrange("p j (c i) -> p c j i", i=4),
+            )
+
+        def regroup_first(i):
+            if not live(i):
+                return
+            xg[i] = work.tile([P, 2, CH * T], BF16, tag="xg", bufs=3, align_bytes=64, name="xg%d" % i)
+            regroup_part(i, nc.scalar.copy, 0, "hsi", 0, CH)
+            regroup_part(i, nc.vector.tensor_copy, 1, "msi", 0, VS)
+
+        def regroup_second(i):
+            if not live(i):
+                return
+            regroup_part(i, nc.scalar.copy, 1, "msi", VS, CH)
+            b = i // PER_B
+            if i % PER_B == PER_B - 1 and b + 2 < B:
+                load("hsi", b + 2, 0, NPIX)
+                load("msi", b + 2, 0, NPIX)
+
+        def quantise_x(i):
+            if not live(i):
+                return
+            xc[i] = work.tile([P, 2, CH], U32, tag="xc", align_bytes=64, name="xc%d" % i)
+            xs[i] = work.tile([P, 2, CH], U8, tag="xs", align_bytes=64, name="xs%d" % i)
+            nc.vector.quantize_mx(
+                out=xc[i][:].rearrange("p s w -> p (s w)").bitcast(FP8X4),
+                scales=xs[i][:].rearrange("p s w -> p (s w)"),
+                in_=xg[i][:].rearrange("p s w -> p (s w)"),
+            )
+
+        def diff_on_vector(i):
+            if not live(i):
+                return
+            mix[i] = work.tile([P, T, CH], F32, tag="mix", name="mix%d" % i)
+            nc.vector.tensor_tensor(
+                out=mix[i][:, TPE:, :], in0=planes("a1", i)[:, TPE:, :], in1=planes("a2", i)[:, TPE:, :], op=ALU.subtract
+            )
+
+        def diff_on_tensor(i):
+            if not live(i):
+                return
+            for t in range(TPE):
+                dps[(i, t)] = psum.tile([P, CH], F32, tag="dps", name="dps%d_%d" % (i, t))
+                nc.tensor.matmul(out=dps[(i, t)][:], lhsT=ident_b[:], rhs=planes("a1", i)[:, t, :], start=True, stop=False)
+                nc.tensor.matmul(out=dps[(i, t)][:], lhsT=minus_b[:], rhs=planes("a2", i)[:, t, :], start=False, stop=True)
+
+        def stage1(i):
+            if not live(i):
+                return
+            for t in range(T):
+                acc1[(i, t)] = psum.tile([P, CH], F32, tag="s1", bufs=4, name="s1_%d_%d" % (i, t))
+                for s in range(2):
+                    k = 2 * t + s
+                    nc.tensor.matmul_mx(
+                        out=acc1[(i, t)][:],
+                        lhsT=wgc[:, k * P : (k + 1) * P].bitcast(FP8X4),
+                        lhsT_scale=wgs[:, k * P : (k + 1) * P],
+                        rhs=xc[i][:, s, :].bitcast(FP8X4),
+                        rhs_scale=xs[i][:, s, :],
+                        start=(s == 0),
+                        stop=(s == 1),
+                    )
+
+        def sigmoid(i):
+            if not live(i):
+                return
+            gate[i] = work.tile([P, T, CH], F32, tag="gate", name="gate%d" % i)
+            for t in range(T):
+                nc.scalar.activation(
+                    out=gate[i][:, t, :], in_=acc1[(i, t)][:], func=ACT.Sigmoid, bias=bgf[:, t : t + 1], scale=1.0
+                )
+
+        def products(i):
+            if not live(i):
+                return
+            for t in range(TPE):
+                nc.vector.tensor_tensor(out=mix[i][:, t, :], in0=gate[i][:, t, :], in1=dps[(i, t)][:], op=ALU.mult)
+            nc.vector.tensor_tensor(out=mix[i][:, TPE:, :], in0=gate[i][:, TPE:, :], in1=mix[i][:, TPE:, :], op=ALU.mult)
+
+        def fuse(i):
+            if not live(i):
+                return
+            fg[i] = work.tile([P, CH * T], BF16, tag="fg", align_bytes=64, name="fg%d" % i)
+            nc.vector.tensor_tensor(
+                out=fg[i][:].rearrange("p (c i t) -> p c t i", i=4, t=T),
+                in0=mix[i][:].rearrange("p t (c i) -> p c t i", i=4),
+                in1=planes("a2", i).rearrange("p t (c i) -> p c t i", i=4),
+                op=ALU.add,
+            )
+
+        def quantise_f(i):
+            if not live(i):
+                return
+            fc[i] = work.tile([P, CH], U32, tag="fc", align_bytes=64, name="fc%d" % i)
+            fs[i] = work.tile([P, CH], U8, tag="fs", align_bytes=64, name="fs%d" % i)
+            nc.vector.quantize_mx(out=fc[i][:].bitcast(FP8X4), scales=fs[i][:], in_=fg[i][:])
+
+        def stage2(i, t):
+            spare = i == NCH - 1 and t >= 2
+            acc2[(i, t)] = psum.tile(
+                [P, CH], F32, tag="s1" if spare else "s2", bufs=4 if spare else 2, name="s2_%d_%d" % (i, t)
+            )
+            nc.tensor.matmul_mx(
+                out=acc2[(i, t)][:],
+                lhsT=wpc[:, t * P : (t + 1) * P].bitcast(FP8X4),
+                lhsT_scale=wps[:, t * P : (t + 1) * P],
+                rhs=fc[i][:].bitcast(FP8X4),
+                rhs_scale=fs[i][:],
+                start=True,
+                stop=True,
+            )
+
+        def stage2_first(i):
+            if not live(i):
+                return
+            for t in range(T if i == NCH - 1 else 2):
+                stage2(i, t)
+
+        def add_bias(i, t):
+            if i == NCH - 1 and t % 2 == 1:
+                nc.vector.tensor_scalar_add(out=y[i][:, t, :], in0=acc2[(i, t)][:], scalar1=bpf[:, t : t + 1])
+            else:
+                nc.scalar.activation(
+                    out=y[i][:, t, :], in_=acc2[(i, t)][:], func=ACT.Identity, bias=bpf[:, t : t + 1], scale=1.0
+                )
+
+        def store(i, queue, t_lo, t_hi):
+            lo = (i % PER_B) * CH
+            queue.dma_start(
+                out=out[i // PER_B].rearrange("(p t) h w -> p t (h w)", t=T)[:, t_lo:t_hi, lo : lo + CH],
+                in_=y[i][:, t_lo:t_hi, :],
+            )
+
+        def finish_first(i):
+            if not live(i):
+                return
+            y[i] = work.tile([P, T, CH], F32, tag="y", bufs=3, name="y%d" % i)
+            for t in range(2):
+                add_bias(i, t)
+                if i < NCH - 1:
+                    stage2(i, t + 2)
+            if i == NCH - 1:
+                store(i, nc.sync, 0, 2)
+
+        def finish_second(i):
+            if not live(i):
+                return
+            for t in range(2, T):
+                add_bias(i, t)
+            if i == NCH - 1:
+                store(i, nc.scalar, 2, T)
+            else:
+                store(i, nc.scalar, 0, T)
+
+        def prepare_weight(raw_w, passes, label, tag, bufs, copy):
+            combos = T * passes
+            words = raw_w[:].bitcast(F32).rearrange("m (t c p u) -> m t c p u", t=T, c=passes, p=P, u=2)
             grouped = const.tile([P, combos * P * 4], BF16, align_bytes=64, name=label + "_grouped")
             gwords = grouped[:].bitcast(F32).rearrange("p (k m u) -> p k m u", k=combos, m=P, u=2)
             codes = const.tile([P, combos * P], U32, align_bytes=64, name=label + "_codes")
             scales = const.tile([P, combos * P], U8, align_bytes=64, name=label + "_scales")
             for bank in range(combos // 2):
-                tp = psum.tile([P, 4, P], F32, tag="tp", bufs=2, name="%s_tp%d" % (label, bank))
+                tp = psum.tile([P, 4, P], F32, tag=tag, bufs=bufs, name="%s_tp%d" % (label, bank))
                 for kk in range(2):
                     k = 2 * bank + kk
                     for u in range(2):
                         nc.tensor.transpose(
-                            out=tp[:, 2 * kk + u, :],
-                            in_=words[:, k // passes, k % passes, :, u],
-                            identity=ident[:],
+                            out=tp[:, 2 * kk + u, :], in_=words[:, k // passes, k % passes, :, u], identity=ident[:]
                         )
-                src = tp[:].rearrange("p (k u) m -> p k m u", k=2, u=2)
-                dst = gwords[:, 2 * bank : 2 * bank + 2, :, :]
-                if bank % 2 == 0:
-                    nc.vector.tensor_copy(out=dst, in_=src)
-                else:
-                    nc.scalar.copy(out=dst, in_=src)
+                copy(out=gwords[:, 2 * bank : 2 * bank + 2, :, :], in_=tp[:].rearrange("p (k u) m -> p k m u", k=2, u=2))
             for half in range(combos // 4):
                 nc.vector.quantize_mx(
                     out=codes[:, half * 512 : (half + 1) * 512].bitcast(FP8X4),
@@ -93,78 +234,65 @@ def tile_crossattentionfusion_pa_t_kernel(tc, hsi, msi, att1, att2, wg, bg, wp, 
                 )
             return codes, scales
 
-        wgc, wgs = prepare_weight(wg_raw, 2, "wg")
-        wpc, wps = prepare_weight(wp_raw, 1, "wp")
+        bg_raw = const.tile([P, T], BF16)
+        bp_raw = const.tile([P, T], BF16)
+        nc.scalar.dma_start(out=bg_raw[:], in_=bg.rearrange("(p t) -> p t", t=T))
+        nc.scalar.dma_start(out=bp_raw[:], in_=bp.rearrange("(p t) -> p t", t=T))
+        wg_raw = const.tile([P, T * 2 * C], BF16)
+        wp_raw = const.tile([P, T * C], BF16)
+        load("hsi", 0, 0, CH)
+        load("msi", 0, 0, CH)
+        nc.sync.dma_start(out=wp_raw[:], in_=wp.rearrange("(m t) k -> m (t k)", t=T))
+        nc.sync.dma_start(out=wg_raw[:], in_=wg.rearrange("(m t) k -> m (t k)", t=T))
+        load("hsi", 0, CH, NPIX)
+        load("msi", 0, CH, NPIX)
+        load("a1", 0, 0, CH)
+        load("a2", 0, 0, CH)
+        load("a1", 0, CH, NPIX)
+        load("a2", 0, CH, NPIX)
+        for name in ("hsi", "msi", "a1", "a2"):
+            load(name, 1, 0, NPIX)
 
-        for b in range(B):
-            if b + 1 < B:
-                load_batch(b + 1)
-            out_b = out[b].rearrange("(p t) h w -> p t (h w)", t=T)
-            for h in range(NCHUNK):
-                cols = slice(h * CH, (h + 1) * CH)
+        warm = const.tile([P, 1], F32)
+        nc.vector.memset(warm[:], 0.0)
+        warm2 = const.tile([P, 1], F32)
+        nc.scalar.activation(out=warm2[:], in_=warm[:], func=ACT.Sigmoid)
+        ident = const.tile([P, P], F32)
+        make_identity(nc, ident[:])
+        ident_b = const.tile([P, P], BF16)
+        make_identity(nc, ident_b[:])
+        minus_b = const.tile([P, P], BF16)
+        nc.vector.tensor_scalar_mul(out=minus_b[:], in0=ident_b[:], scalar1=-1.0)
+        bgf = const.tile([P, T], F32)
+        bpf = const.tile([P, T], F32)
+        nc.vector.tensor_copy(out=bgf[:], in_=bg_raw[:])
+        nc.vector.tensor_copy(out=bpf[:], in_=bp_raw[:])
 
-                def plane_view(name):
-                    return raws[(name, b)][:].rearrange("p (t n) -> p t n", t=T)[:, :, cols]
+        regroup_first(0)
+        regroup_second(0)
+        wpc, wps = prepare_weight(wp_raw, 1, "wp", "s2", 2, nc.vector.tensor_copy)
+        quantise_x(0)
+        wgc, wgs = prepare_weight(wg_raw, 2, "wg", "s1", 4, nc.scalar.copy)
+        regroup_first(1)
+        regroup_second(1)
+        diff_on_vector(0)
+        diff_on_tensor(0)
+        stage1(0)
 
-                xg = work.tile([P, 2, CH * T], BF16, align_bytes=64)
-                for s, name in enumerate(("hsi", "msi")):
-                    nc.scalar.copy(
-                        out=xg[:, s, :].rearrange("p (c i j) -> p c j i", i=4, j=T),
-                        in_=plane_view(name).rearrange("p j (c i) -> p c j i", i=4),
-                    )
-                xc = work.tile([P, 2, CH], U32, align_bytes=64)
-                xs = work.tile([P, 2, CH], U8, align_bytes=64)
-                nc.vector.quantize_mx(
-                    out=xc[:].rearrange("p s w -> p (s w)").bitcast(FP8X4),
-                    scales=xs[:].rearrange("p s w -> p (s w)"),
-                    in_=xg[:].rearrange("p s w -> p (s w)"),
-                )
-                d = work.tile([P, T, CH], F32)
-                nc.vector.tensor_tensor(out=d[:], in0=plane_view("a1"), in1=plane_view("a2"), op=ALU.subtract)
-
-                g = work2.tile([P, T, CH], F32)
-                for t in range(T):
-                    acc = psum.tile([P, CH], F32, tag="s1")
-                    for s in range(2):
-                        k = 2 * t + s
-                        nc.tensor.matmul_mx(
-                            out=acc[:],
-                            lhsT=wgc[:, k * P : (k + 1) * P].bitcast(FP8X4),
-                            lhsT_scale=wgs[:, k * P : (k + 1) * P],
-                            rhs=xc[:, s, :].bitcast(FP8X4),
-                            rhs_scale=xs[:, s, :],
-                            start=(s == 0),
-                            stop=(s == 1),
-                        )
-                    nc.scalar.activation(
-                        out=g[:, t, :], in_=acc[:], func=ACT.Sigmoid, bias=bgf[:, t : t + 1], scale=1.0
-                    )
-
-                nc.vector.tensor_tensor(out=d[:], in0=g[:], in1=d[:], op=ALU.mult)
-                fg = work2.tile([P, CH * T], BF16, align_bytes=64)
-                nc.vector.tensor_tensor(
-                    out=fg[:].rearrange("p (c i t) -> p c t i", i=4, t=T),
-                    in0=d[:].rearrange("p t (c i) -> p c t i", i=4),
-                    in1=plane_view("a2").rearrange("p t (c i) -> p c t i", i=4),
-                    op=ALU.add,
-                )
-                fc = work2.tile([P, CH], U32, align_bytes=64)
-                fs = work2.tile([P, CH], U8, align_bytes=64)
-                nc.vector.quantize_mx(out=fc[:].bitcast(FP8X4), scales=fs[:], in_=fg[:])
-
-                y = work.tile([P, T, CH], F32)
-                for t in range(T):
-                    acc2 = psum.tile([P, CH], F32, tag="s2")
-                    nc.tensor.matmul_mx(
-                        out=acc2[:],
-                        lhsT=wpc[:, t * P : (t + 1) * P].bitcast(FP8X4),
-                        lhsT_scale=wps[:, t * P : (t + 1) * P],
-                        rhs=fc[:].bitcast(FP8X4),
-                        rhs_scale=fs[:],
-                        start=True,
-                        stop=True,
-                    )
-                    nc.scalar.activation(
-                        out=y[:, t, :], in_=acc2[:], func=ACT.Identity, bias=bpf[:, t : t + 1], scale=1.0
-                    )
-                nc.scalar.dma_start(out=out_b[:, :, cols], in_=y[:])
+        for i in range(NCH + 1):
+            quantise_x(i + 1)
+            sigmoid(i)
+            stage1(i + 1)
+            products(i)
+            diff_on_tensor(i + 1)
+            regroup_first(i + 2)
+            finish_first(i - 1)
+            regroup_second(i + 2)
+            finish_second(i - 1)
+            fuse(i)
+            if i % PER_B == PER_B - 1 and i // PER_B + 2 < B:
+                load("a1", i // PER_B + 2, 0, NPIX)
+                load("a2", i // PER_B + 2, 0, NPIX)
+            diff_on_vector(i + 1)
+            quantise_f(i)
+            stage2_first(i)

@@ -210,13 +210,11 @@ def tile_crossattentionfusion_pa_t_kernel(tc, hsi, msi, att1, att2, wg, bg, wp, 
             else:
                 store(i, nc.scalar, 0, T)
 
-        def prepare_weight(raw_w, passes, label, tag, bufs, copy):
+        def transpose_weight(raw_w, passes, label, tag, bufs):
             combos = T * passes
             words = raw_w[:].bitcast(F32).rearrange("m (t c p u) -> m t c p u", t=T, c=passes, p=P, u=2)
             grouped = const.tile([P, combos * P * 4], BF16, align_bytes=64, name=label + "_grouped")
             gwords = grouped[:].bitcast(F32).rearrange("p (k m u) -> p k m u", k=combos, m=P, u=2)
-            codes = const.tile([P, combos * P], U32, align_bytes=64, name=label + "_codes")
-            scales = const.tile([P, combos * P], U8, align_bytes=64, name=label + "_scales")
             for bank in range(combos // 2):
                 tp = psum.tile([P, 4, P], F32, tag=tag, bufs=bufs, name="%s_tp%d" % (label, bank))
                 for kk in range(2):
@@ -225,7 +223,15 @@ def tile_crossattentionfusion_pa_t_kernel(tc, hsi, msi, att1, att2, wg, bg, wp, 
                         nc.tensor.transpose(
                             out=tp[:, 2 * kk + u, :], in_=words[:, k // passes, k % passes, :, u], identity=ident[:]
                         )
-                copy(out=gwords[:, 2 * bank : 2 * bank + 2, :, :], in_=tp[:].rearrange("p (k u) m -> p k m u", k=2, u=2))
+                nc.vector.tensor_copy(
+                    out=gwords[:, 2 * bank : 2 * bank + 2, :, :], in_=tp[:].rearrange("p (k u) m -> p k m u", k=2, u=2)
+                )
+            return grouped
+
+        def quantise_weight(grouped, passes, label):
+            combos = T * passes
+            codes = const.tile([P, combos * P], U32, align_bytes=64, name=label + "_codes")
+            scales = const.tile([P, combos * P], U8, align_bytes=64, name=label + "_scales")
             for half in range(combos // 4):
                 nc.vector.quantize_mx(
                     out=codes[:, half * 512 : (half + 1) * 512].bitcast(FP8X4),
@@ -240,18 +246,22 @@ def tile_crossattentionfusion_pa_t_kernel(tc, hsi, msi, att1, att2, wg, bg, wp, 
         nc.scalar.dma_start(out=bp_raw[:], in_=bp.rearrange("(p t) -> p t", t=T))
         wg_raw = const.tile([P, T * 2 * C], BF16)
         wp_raw = const.tile([P, T * C], BF16)
+        wg_rows = wg.rearrange("(m t) k -> m (t k)", t=T)
+        nc.sync.dma_start(out=wg_raw[:, : T * C], in_=wg_rows[:, : T * C])
+        nc.sync.dma_start(out=wg_raw[:, T * C :], in_=wg_rows[:, T * C :])
+        nc.sync.dma_start(out=wp_raw[:], in_=wp.rearrange("(m t) k -> m (t k)", t=T))
         load("hsi", 0, 0, CH)
         load("msi", 0, 0, CH)
-        nc.sync.dma_start(out=wp_raw[:], in_=wp.rearrange("(m t) k -> m (t k)", t=T))
-        nc.sync.dma_start(out=wg_raw[:], in_=wg.rearrange("(m t) k -> m (t k)", t=T))
         load("hsi", 0, CH, NPIX)
         load("msi", 0, CH, NPIX)
         load("a1", 0, 0, CH)
         load("a2", 0, 0, CH)
+        load("hsi", 1, 0, NPIX)
+        load("msi", 1, 0, NPIX)
         load("a1", 0, CH, NPIX)
         load("a2", 0, CH, NPIX)
-        for name in ("hsi", "msi", "a1", "a2"):
-            load(name, 1, 0, NPIX)
+        load("a1", 1, 0, NPIX)
+        load("a2", 1, 0, NPIX)
 
         warm = const.tile([P, 1], F32)
         nc.vector.memset(warm[:], 0.0)
@@ -263,16 +273,18 @@ def tile_crossattentionfusion_pa_t_kernel(tc, hsi, msi, att1, att2, wg, bg, wp, 
         make_identity(nc, ident_b[:])
         minus_b = const.tile([P, P], BF16)
         nc.vector.tensor_scalar_mul(out=minus_b[:], in0=ident_b[:], scalar1=-1.0)
+
+        wg_grouped = transpose_weight(wg_raw, 2, "wg", "s1", 4)
+        wgc, wgs = quantise_weight(wg_grouped, 2, "wg")
         bgf = const.tile([P, T], F32)
         bpf = const.tile([P, T], F32)
         nc.vector.tensor_copy(out=bgf[:], in_=bg_raw[:])
         nc.vector.tensor_copy(out=bpf[:], in_=bp_raw[:])
-
+        wp_grouped = transpose_weight(wp_raw, 1, "wp", "s2", 2)
         regroup_first(0)
+        wpc, wps = quantise_weight(wp_grouped, 1, "wp")
         regroup_second(0)
-        wpc, wps = prepare_weight(wp_raw, 1, "wp", "s2", 2, nc.vector.tensor_copy)
         quantise_x(0)
-        wgc, wgs = prepare_weight(wg_raw, 2, "wg", "s1", 4, nc.scalar.copy)
         regroup_first(1)
         regroup_second(1)
         diff_on_vector(0)

@@ -19,8 +19,9 @@ T = 4
 CH = 512
 PER_B = NPIX // CH
 NCH = B * PER_B
-VS = 256
+VS = 128
 TPE = 2
+EXTRA = 3
 
 FLOPS = 2 * B * NPIX * (2 * C * C + C * C)
 
@@ -40,6 +41,9 @@ def tile_crossattentionfusion_pa_t_kernel(tc, hsi, msi, att1, att2, wg, bg, wp, 
 
         def live(i):
             return 0 <= i < NCH
+
+        def on_tensor(i):
+            return TPE + 1 if i >= NCH - EXTRA else TPE
 
         def load(name, b, lo, hi):
             if (name, b) not in raw:
@@ -89,18 +93,26 @@ def tile_crossattentionfusion_pa_t_kernel(tc, hsi, msi, att1, att2, wg, bg, wp, 
         def diff_on_vector(i):
             if not live(i):
                 return
+            lo = on_tensor(i)
             mix[i] = work.tile([P, T, CH], F32, tag="mix", name="mix%d" % i)
             nc.vector.tensor_tensor(
-                out=mix[i][:, TPE:, :], in0=planes("a1", i)[:, TPE:, :], in1=planes("a2", i)[:, TPE:, :], op=ALU.subtract
+                out=mix[i][:, lo:, :], in0=planes("a1", i)[:, lo:, :], in1=planes("a2", i)[:, lo:, :], op=ALU.subtract
             )
+
+        def diff_plane(i, t, tag, bufs):
+            dps[(i, t)] = psum.tile([P, CH], F32, tag=tag, bufs=bufs, name="dps%d_%d" % (i, t))
+            nc.tensor.matmul(out=dps[(i, t)][:], lhsT=ident_b[:], rhs=planes("a1", i)[:, t, :], start=True, stop=False)
+            nc.tensor.matmul(out=dps[(i, t)][:], lhsT=minus_b[:], rhs=planes("a2", i)[:, t, :], start=False, stop=True)
 
         def diff_on_tensor(i):
             if not live(i):
                 return
             for t in range(TPE):
-                dps[(i, t)] = psum.tile([P, CH], F32, tag="dps", name="dps%d_%d" % (i, t))
-                nc.tensor.matmul(out=dps[(i, t)][:], lhsT=ident_b[:], rhs=planes("a1", i)[:, t, :], start=True, stop=False)
-                nc.tensor.matmul(out=dps[(i, t)][:], lhsT=minus_b[:], rhs=planes("a2", i)[:, t, :], start=False, stop=True)
+                diff_plane(i, t, "dps", 2)
+
+        def diff_late(i):
+            if live(i) and on_tensor(i) > TPE:
+                diff_plane(i, TPE, "s1", 4)
 
         def stage1(i):
             if not live(i):
@@ -131,9 +143,10 @@ def tile_crossattentionfusion_pa_t_kernel(tc, hsi, msi, att1, att2, wg, bg, wp, 
         def products(i):
             if not live(i):
                 return
-            for t in range(TPE):
+            lo = on_tensor(i)
+            for t in range(lo):
                 nc.vector.tensor_tensor(out=mix[i][:, t, :], in0=gate[i][:, t, :], in1=dps[(i, t)][:], op=ALU.mult)
-            nc.vector.tensor_tensor(out=mix[i][:, TPE:, :], in0=gate[i][:, TPE:, :], in1=mix[i][:, TPE:, :], op=ALU.mult)
+            nc.vector.tensor_tensor(out=mix[i][:, lo:, :], in0=gate[i][:, lo:, :], in1=mix[i][:, lo:, :], op=ALU.mult)
 
         def fuse(i):
             if not live(i):
@@ -197,17 +210,17 @@ def tile_crossattentionfusion_pa_t_kernel(tc, hsi, msi, att1, att2, wg, bg, wp, 
                 add_bias(i, t)
                 if i < NCH - 1:
                     stage2(i, t + 2)
-            if i == NCH - 1:
-                store(i, nc.sync, 0, 2)
+                else:
+                    store(i, nc.sync, t, t + 1)
 
         def finish_second(i):
             if not live(i):
                 return
             for t in range(2, T):
                 add_bias(i, t)
-            if i == NCH - 1:
-                store(i, nc.scalar, 2, T)
-            else:
+                if i == NCH - 1:
+                    store(i, nc.sync, t, t + 1)
+            if i < NCH - 1:
                 store(i, nc.scalar, 0, T)
 
         def transpose_weight(raw_w, passes, label, tag, bufs):
@@ -294,8 +307,9 @@ def tile_crossattentionfusion_pa_t_kernel(tc, hsi, msi, att1, att2, wg, bg, wp, 
         for i in range(NCH + 1):
             quantise_x(i + 1)
             sigmoid(i)
-            stage1(i + 1)
+            diff_late(i)
             products(i)
+            stage1(i + 1)
             diff_on_tensor(i + 1)
             regroup_first(i + 2)
             finish_first(i - 1)

@@ -19,7 +19,7 @@ T = 4
 CH = 512
 PER_B = NPIX // CH
 NCH = B * PER_B
-VS = 128
+VS = 192
 TPE = 2
 EXTRA = 3
 
@@ -41,6 +41,9 @@ def tile_crossattentionfusion_pa_t_kernel(tc, hsi, msi, att1, att2, wg, bg, wp, 
 
         def live(i):
             return 0 <= i < NCH
+
+        def vector_share(i):
+            return CH if i < 2 else VS
 
         def on_tensor(i):
             return TPE + 1 if i >= NCH - EXTRA else TPE
@@ -68,12 +71,13 @@ def tile_crossattentionfusion_pa_t_kernel(tc, hsi, msi, att1, att2, wg, bg, wp, 
                 return
             xg[i] = work.tile([P, 2, CH * T], BF16, tag="xg", bufs=3, align_bytes=64, name="xg%d" % i)
             regroup_part(i, nc.scalar.copy, 0, "hsi", 0, CH)
-            regroup_part(i, nc.vector.tensor_copy, 1, "msi", 0, VS)
+            regroup_part(i, nc.vector.tensor_copy, 1, "msi", 0, vector_share(i))
 
         def regroup_second(i):
             if not live(i):
                 return
-            regroup_part(i, nc.scalar.copy, 1, "msi", VS, CH)
+            if vector_share(i) < CH:
+                regroup_part(i, nc.scalar.copy, 1, "msi", vector_share(i), CH)
             b = i // PER_B
             if i % PER_B == PER_B - 1 and b + 2 < B:
                 load("hsi", b + 2, 0, NPIX)
@@ -301,8 +305,8 @@ def tile_crossattentionfusion_pa_t_kernel(tc, hsi, msi, att1, att2, wg, bg, wp, 
         regroup_first(1)
         regroup_second(1)
         diff_on_vector(0)
-        diff_on_tensor(0)
         stage1(0)
+        diff_on_tensor(0)
 
         for i in range(NCH + 1):
             quantise_x(i + 1)

@@ -225,9 +225,9 @@ def tile_crossattentionfusion_pa_t_kernel(tc, hsi, msi, att1, att2, wg, bg, wp, 
                 if i == NCH - 1:
                     store(i, nc.sync, t, t + 1)
             if i < NCH - 1:
-                store(i, nc.scalar, 0, T)
+                store(i, nc.sync, 0, T)
 
-        def transpose_weight(raw_w, passes, label, tag, bufs):
+        def transpose_weight(raw_w, passes, label, tag, bufs, copy):
             combos = T * passes
             words = raw_w[:].bitcast(F32).rearrange("m (t c p u) -> m t c p u", t=T, c=passes, p=P, u=2)
             grouped = const.tile([P, combos * P * 4], BF16, align_bytes=64, name=label + "_grouped")
@@ -240,9 +240,7 @@ def tile_crossattentionfusion_pa_t_kernel(tc, hsi, msi, att1, att2, wg, bg, wp, 
                         nc.tensor.transpose(
                             out=tp[:, 2 * kk + u, :], in_=words[:, k // passes, k % passes, :, u], identity=ident[:]
                         )
-                nc.vector.tensor_copy(
-                    out=gwords[:, 2 * bank : 2 * bank + 2, :, :], in_=tp[:].rearrange("p (k u) m -> p k m u", k=2, u=2)
-                )
+                copy(out=gwords[:, 2 * bank : 2 * bank + 2, :, :], in_=tp[:].rearrange("p (k u) m -> p k m u", k=2, u=2))
             return grouped
 
         def quantise_weight(grouped, passes, label):
@@ -291,13 +289,13 @@ def tile_crossattentionfusion_pa_t_kernel(tc, hsi, msi, att1, att2, wg, bg, wp, 
         minus_b = const.tile([P, P], BF16)
         nc.vector.tensor_scalar_mul(out=minus_b[:], in0=ident_b[:], scalar1=-1.0)
 
-        wg_grouped = transpose_weight(wg_raw, 2, "wg", "s1", 4)
+        wg_grouped = transpose_weight(wg_raw, 2, "wg", "s1", 4, nc.scalar.copy)
         wgc, wgs = quantise_weight(wg_grouped, 2, "wg")
         bgf = const.tile([P, T], F32)
         bpf = const.tile([P, T], F32)
         nc.vector.tensor_copy(out=bgf[:], in_=bg_raw[:])
         nc.vector.tensor_copy(out=bpf[:], in_=bp_raw[:])
-        wp_grouped = transpose_weight(wp_raw, 1, "wp", "s2", 2)
+        wp_grouped = transpose_weight(wp_raw, 1, "wp", "s2", 2, nc.vector.tensor_copy)
         regroup_first(0)
         wpc, wps = quantise_weight(wp_grouped, 1, "wp")
         regroup_second(0)

@@ -157,9 +157,9 @@ def tile_crossattentionfusion_pa_t_kernel(tc, hsi, msi, att1, att2, wg, bg, wp, 
                 return
             fg[i] = work.tile([P, CH * T], BF16, tag="fg", align_bytes=64, name="fg%d" % i)
             nc.vector.tensor_tensor(
-                out=fg[i][:].rearrange("p (c i t) -> p c t i", i=4, t=T),
-                in0=mix[i][:].rearrange("p t (c i) -> p c t i", i=4),
-                in1=planes("a2", i).rearrange("p t (c i) -> p c t i", i=4),
+                out=fg[i][:].rearrange("p (n t) -> p n t", t=T),
+                in0=mix[i][:].rearrange("p t n -> p n t"),
+                in1=planes("a2", i).rearrange("p t n -> p n t"),
                 op=ALU.add,
             )
 

@@ -157,9 +157,9 @@ def tile_crossattentionfusion_pa_t_kernel(tc, hsi, msi, att1, att2, wg, bg, wp, 
                 return
             fg[i] = work.tile([P, CH * T], BF16, tag="fg", align_bytes=64, name="fg%d" % i)
             nc.vector.tensor_tensor(
-                out=fg[i][:].rearrange("p (n t) -> p n t", t=T),
-                in0=mix[i][:].rearrange("p t n -> p n t"),
-                in1=planes("a2", i).rearrange("p t n -> p n t"),
+                out=fg[i][:].rearrange("p (c i t) -> p c t i", i=8, t=T),
+                in0=mix[i][:].rearrange("p t (c i) -> p c t i", i=8),
+                in1=planes("a2", i).rearrange("p t (c i) -> p c t i", i=8),
                 op=ALU.add,
             )
 

@@ -21,6 +21,8 @@ PER_B = NPIX // CH
 NCH = B * PER_B
 VS = 192
 TPE = 2
+GP = 3
+ORDER = (3, 0, 1, 2)
 EXTRA = 3
 
 FLOPS = 2 * B * NPIX * (2 * C * C + C * C)
@@ -94,13 +96,13 @@ def tile_crossattentionfusion_pa_t_kernel(tc, hsi, msi, att1, att2, wg, bg, wp, 
                 in_=xg[i][:].rearrange("p s w -> p (s w)"),
             )
 
-        def diff_on_vector(i):
-            if not live(i):
+        def diff_on_vector(i, lo, hi):
+            if not live(i) or lo >= hi:
                 return
-            lo = on_tensor(i)
-            mix[i] = work.tile([P, T, CH], F32, tag="mix", name="mix%d" % i)
+            if i not in mix:
+                mix[i] = work.tile([P, T, CH], F32, tag="mix", name="mix%d" % i)
             nc.vector.tensor_tensor(
-                out=mix[i][:, lo:, :], in0=planes("a1", i)[:, lo:, :], in1=planes("a2", i)[:, lo:, :], op=ALU.subtract
+                out=mix[i][:, lo:hi, :], in0=planes("a1", i)[:, lo:hi, :], in1=planes("a2", i)[:, lo:hi, :], op=ALU.subtract
             )
 
         def diff_plane(i, t, tag, bufs):
@@ -121,7 +123,7 @@ def tile_crossattentionfusion_pa_t_kernel(tc, hsi, msi, att1, att2, wg, bg, wp, 
         def stage1(i):
             if not live(i):
                 return
-            for t in range(T):
+            for t in ORDER:
                 acc1[(i, t)] = psum.tile([P, CH], F32, tag="s1", bufs=4, name="s1_%d_%d" % (i, t))
                 for s in range(2):
                     k = 2 * t + s
@@ -139,7 +141,7 @@ def tile_crossattentionfusion_pa_t_kernel(tc, hsi, msi, att1, att2, wg, bg, wp, 
             if not live(i):
                 return
             gate[i] = work.tile([P, T, CH], F32, tag="gate", name="gate%d" % i)
-            for t in range(T):
+            for t in ORDER:
                 nc.scalar.activation(
                     out=gate[i][:, t, :], in_=acc1[(i, t)][:], func=ACT.Sigmoid, bias=bgf[:, t : t + 1], scale=1.0
                 )
@@ -148,9 +150,13 @@ def tile_crossattentionfusion_pa_t_kernel(tc, hsi, msi, att1, att2, wg, bg, wp, 
             if not live(i):
                 return
             lo = on_tensor(i)
+            nc.gpsimd.tensor_tensor(out=mix[i][:, GP, :], in0=gate[i][:, GP, :], in1=mix[i][:, GP, :], op=ALU.mult)
             for t in range(lo):
                 nc.vector.tensor_tensor(out=mix[i][:, t, :], in0=gate[i][:, t, :], in1=dps[(i, t)][:], op=ALU.mult)
-            nc.vector.tensor_tensor(out=mix[i][:, lo:, :], in0=gate[i][:, lo:, :], in1=mix[i][:, lo:, :], op=ALU.mult)
+            if lo < GP:
+                nc.vector.tensor_tensor(
+                    out=mix[i][:, lo:GP, :], in0=gate[i][:, lo:GP, :], in1=mix[i][:, lo:GP, :], op=ALU.mult
+                )
 
         def fuse(i):
             if not live(i):
@@ -302,7 +308,7 @@ def tile_crossattentionfusion_pa_t_kernel(tc, hsi, msi, att1, att2, wg, bg, wp, 
         quantise_x(0)
         regroup_first(1)
         regroup_second(1)
-        diff_on_vector(0)
+        diff_on_vector(0, on_tensor(0), GP)
         stage1(0)
         diff_on_tensor(0)
 
@@ -310,6 +316,7 @@ def tile_crossattentionfusion_pa_t_kernel(tc, hsi, msi, att1, att2, wg, bg, wp, 
             quantise_x(i + 1)
             sigmoid(i)
             diff_late(i)
+            diff_on_vector(i, GP, T)
             products(i)
             stage1(i + 1)
             diff_on_tensor(i + 1)
@@ -321,6 +328,6 @@ def tile_crossattentionfusion_pa_t_kernel(tc, hsi, msi, att1, att2, wg, bg, wp, 
             if i % PER_B == PER_B - 1 and i // PER_B + 2 < B:
                 load("a1", i // PER_B + 2, 0, NPIX)
                 load("a2", i // PER_B + 2, 0, NPIX)
-            diff_on_vector(i + 1)
+            diff_on_vector(i + 1, on_tensor(i + 1), GP)
             quantise_f(i)
             stage2_first(i)

@@ -19,7 +19,7 @@ T = 4
 CH = 512
 PER_B = NPIX // CH
 NCH = B * PER_B
-VS = 192
+VS = 256
 TPE = 2
 GP = 3
 ORDER = (3, 0, 1, 2)

@@ -19,7 +19,7 @@ T = 4
 CH = 512
 PER_B = NPIX // CH
 NCH = B * PER_B
-VS = 256
+VS = 152
 TPE = 2
 GP = 3
 ORDER = (3, 0, 1, 2)
@@ -153,6 +153,9 @@ def tile_crossattentionfusion_pa_t_kernel(tc, hsi, msi, att1, att2, wg, bg, wp, 
             nc.gpsimd.tensor_tensor(out=mix[i][:, GP, :], in0=gate[i][:, GP, :], in1=mix[i][:, GP, :], op=ALU.mult)
             for t in range(lo):
                 nc.vector.tensor_tensor(out=mix[i][:, t, :], in0=gate[i][:, t, :], in1=dps[(i, t)][:], op=ALU.mult)
+            if vector_takes(i - 1, 0):
+                y[i - 1] = work.tile([P, T, CH], F32, tag="y", bufs=3, name="y%d" % (i - 1))
+                add_bias(i - 1, 0)
             if lo < GP:
                 nc.vector.tensor_tensor(
                     out=mix[i][:, lo:GP, :], in0=gate[i][:, lo:GP, :], in1=mix[i][:, lo:GP, :], op=ALU.mult
@@ -197,8 +200,11 @@ def tile_crossattentionfusion_pa_t_kernel(tc, hsi, msi, att1, att2, wg, bg, wp, 
             for t in range(T if i == NCH - 1 else 2):
                 stage2(i, t)
 
+        def vector_takes(i, t):
+            return live(i) and ((t == 0 and live(i + 3)) or (i == NCH - 1 and t % 2 == 1))
+
         def add_bias(i, t):
-            if i == NCH - 1 and t % 2 == 1:
+            if vector_takes(i, t):
                 nc.vector.tensor_scalar_add(out=y[i][:, t, :], in0=acc2[(i, t)][:], scalar1=bpf[:, t : t + 1])
             else:
                 nc.scalar.activation(
@@ -214,6 +220,10 @@ def tile_crossattentionfusion_pa_t_kernel(tc, hsi, msi, att1, att2, wg, bg, wp, 
 
         def finish_first(i):
             if not live(i):
+                return
+            if vector_takes(i, 0):
+                add_bias(i, 1)
+                stage2(i, 3)
                 return
             y[i] = work.tile([P, T, CH], F32, tag="y", bufs=3, name="y%d" % i)
             for t in range(2):
@@ -320,6 +330,8 @@ def tile_crossattentionfusion_pa_t_kernel(tc, hsi, msi, att1, att2, wg, bg, wp, 
             products(i)
             stage1(i + 1)
             diff_on_tensor(i + 1)
+            if vector_takes(i - 1, 0):
+                stage2(i - 1, 2)
             regroup_first(i + 2)
             finish_first(i - 1)
             regroup_second(i + 2)

@@ -73,7 +73,10 @@ def tile_crossattentionfusion_pa_t_kernel(tc, hsi, msi, att1, att2, wg, bg, wp, 
                 return
             xg[i] = work.tile([P, 2, CH * T], BF16, tag="xg", bufs=3, align_bytes=64, name="xg%d" % i)
             regroup_part(i, nc.scalar.copy, 0, "hsi", 0, CH)
-            regroup_part(i, nc.vector.tensor_copy, 1, "msi", 0, vector_share(i))
+
+        def regroup_vector(i):
+            if live(i):
+                regroup_part(i, nc.vector.tensor_copy, 1, "msi", 0, vector_share(i))
 
         def regroup_second(i):
             if not live(i):
@@ -313,33 +316,53 @@ def tile_crossattentionfusion_pa_t_kernel(tc, hsi, msi, att1, att2, wg, bg, wp, 
         nc.vector.tensor_copy(out=bpf[:], in_=bp_raw[:])
         wp_grouped = transpose_weight(wp_raw, 1, "wp", "s2", 2, nc.vector.tensor_copy)
         regroup_first(0)
+        regroup_vector(0)
         wpc, wps = quantise_weight(wp_grouped, 1, "wp")
         regroup_second(0)
         quantise_x(0)
         regroup_first(1)
+        regroup_vector(1)
         regroup_second(1)
         diff_on_vector(0, on_tensor(0), GP)
         stage1(0)
         diff_on_tensor(0)
 
+        early_diff = set()
         for i in range(NCH + 1):
-            quantise_x(i + 1)
+            last_regroup = live(i + 2) and on_tensor(i) == GP
+            no_regroup = live(i + 1) and not live(i + 2)
+            if not no_regroup:
+                quantise_x(i + 1)
             sigmoid(i)
             diff_late(i)
-            diff_on_vector(i, GP, T)
+            if i not in early_diff:
+                diff_on_vector(i, GP, T)
             products(i)
+            if no_regroup:
+                finish_first(i - 1)
+                finish_second(i - 1)
+                quantise_x(i + 1)
             stage1(i + 1)
-            diff_on_tensor(i + 1)
             if vector_takes(i - 1, 0):
                 stage2(i - 1, 2)
             regroup_first(i + 2)
-            finish_first(i - 1)
+            if not last_regroup:
+                regroup_vector(i + 2)
+            if not no_regroup:
+                finish_first(i - 1)
+            diff_on_tensor(i + 1)
             regroup_second(i + 2)
-            finish_second(i - 1)
+            if not no_regroup:
+                finish_second(i - 1)
             fuse(i)
             if i % PER_B == PER_B - 1 and i // PER_B + 2 < B:
                 load("a1", i // PER_B + 2, 0, NPIX)
                 load("a2", i // PER_B + 2, 0, NPIX)
+            if last_regroup:
+                regroup_vector(i + 2)
             diff_on_vector(i + 1, on_tensor(i + 1), GP)
+            if no_regroup:
+                diff_on_vector(i + 1, GP, T)
+                early_diff.add(i + 1)
             quantise_f(i)
             stage2_first(i)

@@ -19,7 +19,7 @@ T = 4
 CH = 512
 PER_B = NPIX // CH
 NCH = B * PER_B
-VS = 152
+VS = 304
 TPE = 2
 GP = 3
 ORDER = (3, 0, 1, 2)
@@ -204,7 +204,7 @@ def tile_crossattentionfusion_pa_t_kernel(tc, hsi, msi, att1, att2, wg, bg, wp, 
                 stage2(i, t)
 
         def vector_takes(i, t):
-            return live(i) and ((t == 0 and live(i + 3)) or (i == NCH - 1 and t % 2 == 1))
+            return i == NCH - 1 and t % 2 == 1
 
         def add_bias(i, t):
             if vector_takes(i, t):
@@ -307,62 +307,47 @@ def tile_crossattentionfusion_pa_t_kernel(tc, hsi, msi, att1, att2, wg, bg, wp, 
         make_identity(nc, ident_b[:])
         minus_b = const.tile([P, P], BF16)
         nc.vector.tensor_scalar_mul(out=minus_b[:], in0=ident_b[:], scalar1=-1.0)
-
-        wg_grouped = transpose_weight(wg_raw, 2, "wg", "s1", 4, nc.scalar.copy)
-        wgc, wgs = quantise_weight(wg_grouped, 2, "wg")
         bgf = const.tile([P, T], F32)
         bpf = const.tile([P, T], F32)
         nc.vector.tensor_copy(out=bgf[:], in_=bg_raw[:])
         nc.vector.tensor_copy(out=bpf[:], in_=bp_raw[:])
-        wp_grouped = transpose_weight(wp_raw, 1, "wp", "s2", 2, nc.vector.tensor_copy)
+
+        wg_grouped = transpose_weight(wg_raw, 2, "wg", "s1", 4, nc.scalar.copy)
+        wgc, wgs = quantise_weight(wg_grouped, 2, "wg")
         regroup_first(0)
         regroup_vector(0)
-        wpc, wps = quantise_weight(wp_grouped, 1, "wp")
+        wp_grouped = transpose_weight(wp_raw, 1, "wp", "s2", 2, nc.scalar.copy)
         regroup_second(0)
         quantise_x(0)
         regroup_first(1)
         regroup_vector(1)
         regroup_second(1)
-        diff_on_vector(0, on_tensor(0), GP)
+        wpc, wps = quantise_weight(wp_grouped, 1, "wp")
+        diff_on_vector(0, on_tensor(0), T)
+        quantise_x(1)
         stage1(0)
         diff_on_tensor(0)
+        sigmoid(0)
 
-        early_diff = set()
         for i in range(NCH + 1):
-            last_regroup = live(i + 2) and on_tensor(i) == GP
-            no_regroup = live(i + 1) and not live(i + 2)
-            if not no_regroup:
-                quantise_x(i + 1)
-            sigmoid(i)
-            diff_late(i)
-            if i not in early_diff:
-                diff_on_vector(i, GP, T)
             products(i)
-            if no_regroup:
-                finish_first(i - 1)
-                finish_second(i - 1)
-                quantise_x(i + 1)
-            stage1(i + 1)
+            diff_on_tensor(i + 1)
             if vector_takes(i - 1, 0):
                 stage2(i - 1, 2)
             regroup_first(i + 2)
-            if not last_regroup:
-                regroup_vector(i + 2)
-            if not no_regroup:
-                finish_first(i - 1)
-            diff_on_tensor(i + 1)
+            finish_first(i - 1)
+            if i > 0:
+                quantise_x(i + 1)
+            stage1(i + 1)
+            regroup_vector(i + 2)
             regroup_second(i + 2)
-            if not no_regroup:
-                finish_second(i - 1)
+            finish_second(i - 1)
+            sigmoid(i + 1)
+            diff_late(i + 1)
             fuse(i)
             if i % PER_B == PER_B - 1 and i // PER_B + 2 < B:
                 load("a1", i // PER_B + 2, 0, NPIX)
                 load("a2", i // PER_B + 2, 0, NPIX)
-            if last_regroup:
-                regroup_vector(i + 2)
-            diff_on_vector(i + 1, on_tensor(i + 1), GP)
-            if no_regroup:
-                diff_on_vector(i + 1, GP, T)
-                early_diff.add(i + 1)
+            diff_on_vector(i + 1, on_tensor(i + 1), T)
             quantise_f(i)
             stage2_first(i)

@@ -149,16 +149,19 @@ def tile_crossattentionfusion_pa_t_kernel(tc, hsi, msi, att1, att2, wg, bg, wp, 
                     out=gate[i][:, t, :], in_=acc1[(i, t)][:], func=ACT.Sigmoid, bias=bgf[:, t : t + 1], scale=1.0
                 )
 
+        def pieces(i):
+            return ((0, CH // 2), (CH // 2, CH)) if i == NCH - 1 else ((0, CH),)
+
         def products(i):
             if not live(i):
                 return
             lo = on_tensor(i)
             nc.gpsimd.tensor_tensor(out=mix[i][:, GP, :], in0=gate[i][:, GP, :], in1=mix[i][:, GP, :], op=ALU.mult)
             for t in range(lo):
-                nc.vector.tensor_tensor(out=mix[i][:, t, :], in0=gate[i][:, t, :], in1=dps[(i, t)][:], op=ALU.mult)
-            if vector_takes(i - 1, 0):
-                y[i - 1] = work.tile([P, T, CH], F32, tag="y", bufs=3, name="y%d" % (i - 1))
-                add_bias(i - 1, 0)
+                for a, b in pieces(i) if t == lo - 1 else ((0, CH),):
+                    nc.vector.tensor_tensor(
+                        out=mix[i][:, t, a:b], in0=gate[i][:, t, a:b], in1=dps[(i, t)][:, a:b], op=ALU.mult
+                    )
             if lo < GP:
                 nc.vector.tensor_tensor(
                     out=mix[i][:, lo:GP, :], in0=gate[i][:, lo:GP, :], in1=mix[i][:, lo:GP, :], op=ALU.mult
@@ -168,83 +171,81 @@ def tile_crossattentionfusion_pa_t_kernel(tc, hsi, msi, att1, att2, wg, bg, wp, 
             if not live(i):
                 return
             fg[i] = work.tile([P, CH * T], BF16, tag="fg", align_bytes=64, name="fg%d" % i)
-            nc.vector.tensor_tensor(
-                out=fg[i][:].rearrange("p (c i t) -> p c t i", i=8, t=T),
-                in0=mix[i][:].rearrange("p t (c i) -> p c t i", i=8),
-                in1=planes("a2", i).rearrange("p t (c i) -> p c t i", i=8),
-                op=ALU.add,
-            )
+            for a, b in pieces(i):
+                nc.vector.tensor_tensor(
+                    out=fg[i][:, a * T : b * T].rearrange("p (c i t) -> p c t i", i=8, t=T),
+                    in0=mix[i][:, :, a:b].rearrange("p t (c i) -> p c t i", i=8),
+                    in1=planes("a2", i)[:, :, a:b].rearrange("p t (c i) -> p c t i", i=8),
+                    op=ALU.add,
+                )
 
         def quantise_f(i):
             if not live(i):
                 return
             fc[i] = work.tile([P, CH], U32, tag="fc", align_bytes=64, name="fc%d" % i)
             fs[i] = work.tile([P, CH], U8, tag="fs", align_bytes=64, name="fs%d" % i)
-            nc.vector.quantize_mx(out=fc[i][:].bitcast(FP8X4), scales=fs[i][:], in_=fg[i][:])
+            for a, b in pieces(i):
+                nc.vector.quantize_mx(out=fc[i][:, a:b].bitcast(FP8X4), scales=fs[i][:, a:b], in_=fg[i][:, a * T : b * T])
+                for t in range(T if i == NCH - 1 else 2):
+                    stage2(i, t, a, b)
 
-        def stage2(i, t):
-            spare = i == NCH - 1 and t >= 2
-            acc2[(i, t)] = psum.tile(
-                [P, CH], F32, tag="s1" if spare else "s2", bufs=4 if spare else 2, name="s2_%d_%d" % (i, t)
-            )
+        def bank(i, t, a):
+            if i < NCH - 1 or (a == 0 and t < 2):
+                return "s2", 2
+            if a == 0 or t < 2:
+                return "s1", 4
+            return "dps", 2
+
+        def stage2(i, t, a, b):
+            tag, bufs = bank(i, t, a)
+            acc2[(i, t, a)] = psum.tile([P, b - a], F32, tag=tag, bufs=bufs, name="s2_%d_%d_%d" % (i, t, a))
             nc.tensor.matmul_mx(
-                out=acc2[(i, t)][:],
+                out=acc2[(i, t, a)][:],
                 lhsT=wpc[:, t * P : (t + 1) * P].bitcast(FP8X4),
                 lhsT_scale=wps[:, t * P : (t + 1) * P],
-                rhs=fc[i][:].bitcast(FP8X4),
-                rhs_scale=fs[i][:],
+                rhs=fc[i][:, a:b].bitcast(FP8X4),
+                rhs_scale=fs[i][:, a:b],
                 start=True,
                 stop=True,
             )
 
-        def stage2_first(i):
-            if not live(i):
-                return
-            for t in range(T if i == NCH - 1 else 2):
-                stage2(i, t)
-
-        def vector_takes(i, t):
-            return i == NCH - 1 and t % 2 == 1
-
-        def add_bias(i, t):
-            if vector_takes(i, t):
-                nc.vector.tensor_scalar_add(out=y[i][:, t, :], in0=acc2[(i, t)][:], scalar1=bpf[:, t : t + 1])
+        def add_bias(i, t, a, b, on_vector):
+            if on_vector:
+                nc.vector.tensor_scalar_add(out=y[i][:, t, a:b], in0=acc2[(i, t, a)][:], scalar1=bpf[:, t : t + 1])
             else:
                 nc.scalar.activation(
-                    out=y[i][:, t, :], in_=acc2[(i, t)][:], func=ACT.Identity, bias=bpf[:, t : t + 1], scale=1.0
+                    out=y[i][:, t, a:b], in_=acc2[(i, t, a)][:], func=ACT.Identity, bias=bpf[:, t : t + 1], scale=1.0
                 )
 
-        def store(i, queue, t_lo, t_hi):
+        def store(i, t_lo, t_hi, a, b):
             lo = (i % PER_B) * CH
-            queue.dma_start(
-                out=out[i // PER_B].rearrange("(p t) h w -> p t (h w)", t=T)[:, t_lo:t_hi, lo : lo + CH],
-                in_=y[i][:, t_lo:t_hi, :],
+            nc.sync.dma_start(
+                out=out[i // PER_B].rearrange("(p t) h w -> p t (h w)", t=T)[:, t_lo:t_hi, lo + a : lo + b],
+                in_=y[i][:, t_lo:t_hi, a:b],
             )
 
         def finish_first(i):
             if not live(i):
                 return
-            if vector_takes(i, 0):
-                add_bias(i, 1)
-                stage2(i, 3)
-                return
             y[i] = work.tile([P, T, CH], F32, tag="y", bufs=3, name="y%d" % i)
+            if i == NCH - 1:
+                return
             for t in range(2):
-                add_bias(i, t)
-                if i < NCH - 1:
-                    stage2(i, t + 2)
-                else:
-                    store(i, nc.sync, t, t + 1)
+                add_bias(i, t, 0, CH, False)
+                stage2(i, t + 2, 0, CH)
 
         def finish_second(i):
             if not live(i):
                 return
-            for t in range(2, T):
-                add_bias(i, t)
-                if i == NCH - 1:
-                    store(i, nc.sync, t, t + 1)
             if i < NCH - 1:
-                store(i, nc.sync, 0, T)
+                for t in range(2, T):
+                    add_bias(i, t, 0, CH, False)
+                store(i, 0, T, 0, CH)
+                return
+            for a, b in pieces(i):
+                for t in range(T):
+                    add_bias(i, t, a, b, a > 0 and t < T - 1)
+                    store(i, t, t + 1, a, b)
 
         def transpose_weight(raw_w, passes, label, tag, bufs, copy):
             combos = T * passes
@@ -290,10 +291,12 @@ def tile_crossattentionfusion_pa_t_kernel(tc, hsi, msi, att1, att2, wg, bg, wp, 
         load("msi", 0, CH, NPIX)
         load("a1", 0, 0, CH)
         load("a2", 0, 0, CH)
-        load("hsi", 1, 0, NPIX)
-        load("msi", 1, 0, NPIX)
+        load("hsi", 1, 0, CH)
+        load("msi", 1, 0, CH)
         load("a1", 0, CH, NPIX)
         load("a2", 0, CH, NPIX)
+        load("hsi", 1, CH, NPIX)
+        load("msi", 1, CH, NPIX)
         load("a1", 1, 0, NPIX)
         load("a2", 1, 0, NPIX)
 
@@ -331,14 +334,14 @@ def tile_crossattentionfusion_pa_t_kernel(tc, hsi, msi, att1, att2, wg, bg, wp, 
 
         for i in range(NCH + 1):
             products(i)
+            if i == 0:
+                stage1(i + 1)
             diff_on_tensor(i + 1)
-            if vector_takes(i - 1, 0):
-                stage2(i - 1, 2)
             regroup_first(i + 2)
             finish_first(i - 1)
             if i > 0:
                 quantise_x(i + 1)
-            stage1(i + 1)
+                stage1(i + 1)
             regroup_vector(i + 2)
             regroup_second(i + 2)
             finish_second(i - 1)
@@ -350,4 +353,3 @@ def tile_crossattentionfusion_pa_t_kernel(tc, hsi, msi, att1, att2, wg, bg, wp, 
                 load("a2", i // PER_B + 2, 0, NPIX)
             diff_on_vector(i + 1, on_tensor(i + 1), T)
             quantise_f(i)
-            stage2_first(i)

@@ -291,12 +291,10 @@ def tile_crossattentionfusion_pa_t_kernel(tc, hsi, msi, att1, att2, wg, bg, wp, 
         load("msi", 0, CH, NPIX)
         load("a1", 0, 0, CH)
         load("a2", 0, 0, CH)
-        load("hsi", 1, 0, CH)
-        load("msi", 1, 0, CH)
+        load("hsi", 1, 0, NPIX)
+        load("msi", 1, 0, NPIX)
         load("a1", 0, CH, NPIX)
         load("a2", 0, CH, NPIX)
-        load("hsi", 1, CH, NPIX)
-        load("msi", 1, CH, NPIX)
         load("a1", 1, 0, NPIX)
         load("a2", 1, 0, NPIX)
 

@@ -40,6 +40,7 @@ def tile_crossattentionfusion_pa_t_kernel(tc, hsi, msi, att1, att2, wg, bg, wp, 
 
         raw, xg, xc, xs, gate, mix, dps = {}, {}, {}, {}, {}, {}, {}
         acc1, acc2, fc, fs, fg, y = {}, {}, {}, {}, {}, {}
+        halved = set()
 
         def live(i):
             return 0 <= i < NCH
@@ -53,14 +54,23 @@ def tile_crossattentionfusion_pa_t_kernel(tc, hsi, msi, att1, att2, wg, bg, wp, 
         def load(name, b, lo, hi):
             if (name, b) not in raw:
                 raw[(name, b)] = xin.tile([P, T * NPIX], BF16, tag=name, name="%s%d" % (name, b))
-            nc.sync.dma_start(
-                out=raw[(name, b)][:].rearrange("p (t n) -> p t n", t=T)[:, :, lo:hi],
-                in_=sources[name][b].rearrange("(p t) h w -> p t (h w)", t=T)[:, :, lo:hi],
-            )
+            if hi - lo == NPIX:
+                nc.sync.dma_start(
+                    out=raw[(name, b)][:].rearrange("p (t n) -> p t n", t=T),
+                    in_=sources[name][b].rearrange("(p t) h w -> p t (h w)", t=T),
+                )
+            else:
+                halved.add((name, b))
+                nc.sync.dma_start(
+                    out=raw[(name, b)][:, T * lo : T * hi].rearrange("p (t n) -> p t n", t=T),
+                    in_=sources[name][b].rearrange("(p t) h w -> p t (h w)", t=T)[:, :, lo:hi],
+                )
 
         def planes(name, i):
-            lo = (i % PER_B) * CH
-            return raw[(name, i // PER_B)][:].rearrange("p (t n) -> p t n", t=T)[:, :, lo : lo + CH]
+            b, lo = i // PER_B, (i % PER_B) * CH
+            if (name, b) in halved:
+                return raw[(name, b)][:, T * lo : T * (lo + CH)].rearrange("p (t n) -> p t n", t=T)
+            return raw[(name, b)][:].rearrange("p (t n) -> p t n", t=T)[:, :, lo : lo + CH]
 
         def regroup_part(i, copy, s, name, lo, hi):
             copy(

@@ -162,26 +162,28 @@ def tile_crossattentionfusion_pa_t_kernel(tc, hsi, msi, att1, att2, wg, bg, wp, 
         def pieces(i):
             return ((0, CH // 2), (CH // 2, CH)) if i == NCH - 1 else ((0, CH),)
 
+        def product(i, t, a, b):
+            nc.vector.tensor_tensor(out=mix[i][:, t, a:b], in0=gate[i][:, t, a:b], in1=dps[(i, t)][:, a:b], op=ALU.mult)
+
         def products(i):
             if not live(i):
                 return
             lo = on_tensor(i)
             nc.gpsimd.tensor_tensor(out=mix[i][:, GP, :], in0=gate[i][:, GP, :], in1=mix[i][:, GP, :], op=ALU.mult)
+            if i == NCH - 1:
+                product(i, 0, 0, CH)
+                product(i, 1, 0, CH // 2)
+                product(i, 2, 0, CH // 2)
+                product(i, 1, CH // 2, CH)
+                return
             for t in range(lo):
-                for a, b in pieces(i) if t == lo - 1 else ((0, CH),):
-                    nc.vector.tensor_tensor(
-                        out=mix[i][:, t, a:b], in0=gate[i][:, t, a:b], in1=dps[(i, t)][:, a:b], op=ALU.mult
-                    )
+                product(i, t, 0, CH)
             if lo < GP:
                 nc.vector.tensor_tensor(
                     out=mix[i][:, lo:GP, :], in0=gate[i][:, lo:GP, :], in1=mix[i][:, lo:GP, :], op=ALU.mult
                 )
 
-        def fuse(i):
-            if not live(i):
-                return
-            fg[i] = work.tile([P, CH * T], BF16, tag="fg", align_bytes=64, name="fg%d" % i)
-            for a, b in pieces(i):
+        def fuse_piece(i, a, b):
                 nc.vector.tensor_tensor(
                     out=fg[i][:, a * T : b * T].rearrange("p (c i t) -> p c t i", i=8, t=T),
                     in0=mix[i][:, :, a:b].rearrange("p t (c i) -> p c t i", i=8),
@@ -189,12 +191,24 @@ def tile_crossattentionfusion_pa_t_kernel(tc, hsi, msi, att1, att2, wg, bg, wp, 
                     op=ALU.add,
                 )
 
+        def fuse(i):
+            if not live(i):
+                return
+            fg[i] = work.tile([P, CH * T], BF16, tag="fg", align_bytes=64, name="fg%d" % i)
+            if i == NCH - 1:
+                fuse_piece(i, 0, CH // 2)
+                product(i, 2, CH // 2, CH)
+            else:
+                fuse_piece(i, 0, CH)
+
         def quantise_f(i):
             if not live(i):
                 return
             fc[i] = work.tile([P, CH], U32, tag="fc", align_bytes=64, name="fc%d" % i)
             fs[i] = work.tile([P, CH], U8, tag="fs", align_bytes=64, name="fs%d" % i)
             for a, b in pieces(i):
+                if a > 0:
+                    fuse_piece(i, a, b)
                 nc.vector.quantize_mx(out=fc[i][:, a:b].bitcast(FP8X4), scales=fs[i][:, a:b], in_=fg[i][:, a * T : b * T])
                 for t in range(T if i == NCH - 1 else 2):
                     stage2(i, t, a, b)
@@ -243,6 +257,10 @@ def tile_crossattentionfusion_pa_t_kernel(tc, hsi, msi, att1, att2, wg, bg, wp, 
             for t in range(2):
                 add_bias(i, t, 0, CH, False)
                 stage2(i, t + 2, 0, CH)
+                if i == NCH - 2:
+                    store(i, t, t + 1, 0, CH)
+            if i < NCH - 2:
+                store(i, 0, 2, 0, CH)
 
         def finish_second(i):
             if not live(i):
@@ -250,7 +268,10 @@ def tile_crossattentionfusion_pa_t_kernel(tc, hsi, msi, att1, att2, wg, bg, wp, 
             if i < NCH - 1:
                 for t in range(2, T):
                     add_bias(i, t, 0, CH, False)
-                store(i, 0, T, 0, CH)
+                    if i == NCH - 2:
+                        store(i, t, t + 1, 0, CH)
+                if i < NCH - 2:
+                    store(i, 2, T, 0, CH)
                 return
             for a, b in pieces(i):
                 for t in range(T):

@@ -19,7 +19,7 @@ T = 4
 CH = 512
 PER_B = NPIX // CH
 NCH = B * PER_B
-VS = 304
+VS = 352
 TPE = 2
 GP = 3
 ORDER = (3, 0, 1, 2)

@@ -78,10 +78,13 @@ def tile_crossattentionfusion_pa_t_kernel(tc, hsi, msi, att1, att2, wg, bg, wp, 
                 in_=planes(name, i)[:, :, lo:hi].rearrange("p j (c i) -> p c j i", i=4),
             )
 
+        def regroup_open(i):
+            xg[i] = work.tile([P, 2, CH * T], BF16, tag="xg", bufs=3, align_bytes=64, name="xg%d" % i)
+
         def regroup_first(i):
             if not live(i):
                 return
-            xg[i] = work.tile([P, 2, CH * T], BF16, tag="xg", bufs=3, align_bytes=64, name="xg%d" % i)
+            regroup_open(i)
             regroup_part(i, nc.scalar.copy, 0, "hsi", 0, CH)
 
         def regroup_vector(i):
@@ -315,11 +318,9 @@ def tile_crossattentionfusion_pa_t_kernel(tc, hsi, msi, att1, att2, wg, bg, wp, 
         wg_rows = wg.rearrange("(m t) k -> m (t k)", t=T)
         nc.sync.dma_start(out=wg_raw[:, : T * C], in_=wg_rows[:, : T * C])
         nc.sync.dma_start(out=wg_raw[:, T * C :], in_=wg_rows[:, T * C :])
+        load("hsi", 0, 0, NPIX)
+        load("msi", 0, 0, NPIX)
         nc.sync.dma_start(out=wp_raw[:], in_=wp.rearrange("(m t) k -> m (t k)", t=T))
-        load("hsi", 0, 0, CH)
-        load("msi", 0, 0, CH)
-        load("hsi", 0, CH, NPIX)
-        load("msi", 0, CH, NPIX)
         load("a1", 0, 0, CH)
         load("a2", 0, 0, CH)
         load("hsi", 1, 0, NPIX)
@@ -341,23 +342,24 @@ def tile_crossattentionfusion_pa_t_kernel(tc, hsi, msi, att1, att2, wg, bg, wp, 
         nc.vector.tensor_scalar_mul(out=minus_b[:], in0=ident_b[:], scalar1=-1.0)
         bgf = const.tile([P, T], F32)
         bpf = const.tile([P, T], F32)
-        nc.vector.tensor_copy(out=bgf[:], in_=bg_raw[:])
-        nc.vector.tensor_copy(out=bpf[:], in_=bp_raw[:])
 
         wg_grouped = transpose_weight(wg_raw, 2, "wg", "s1", 4, nc.scalar.copy)
         wgc, wgs = quantise_weight(wg_grouped, 2, "wg")
         regroup_first(0)
-        regroup_vector(0)
-        wp_grouped = transpose_weight(wp_raw, 1, "wp", "s2", 2, nc.scalar.copy)
-        regroup_second(0)
+        regroup_open(1)
+        regroup_part(1, nc.scalar.copy, 0, "hsi", 0, 512)
+        regroup_part(0, nc.vector.tensor_copy, 1, "msi", 0, CH)
+        nc.vector.tensor_copy(out=bgf[:], in_=bg_raw[:])
+        nc.vector.tensor_copy(out=bpf[:], in_=bp_raw[:])
         quantise_x(0)
-        regroup_first(1)
-        regroup_vector(1)
-        regroup_second(1)
+        regroup_part(1, nc.vector.tensor_copy, 1, "msi", 0, CH)
+        load("hsi", 2, 0, NPIX)
+        load("msi", 2, 0, NPIX)
+        wp_grouped = transpose_weight(wp_raw, 1, "wp", "s2", 2, nc.scalar.copy)
         wpc, wps = quantise_weight(wp_grouped, 1, "wp")
-        diff_on_vector(0, on_tensor(0), T)
         quantise_x(1)
         stage1(0)
+        diff_on_vector(0, on_tensor(0), T)
         diff_on_tensor(0)
         sigmoid(0)
 

@@ -19,7 +19,7 @@ T = 4
 CH = 512
 PER_B = NPIX // CH
 NCH = B * PER_B
-VS = 352
+VS = 368
 TPE = 2
 GP = 3
 ORDER = (3, 0, 1, 2)
@@ -46,7 +46,7 @@ def tile_crossattentionfusion_pa_t_kernel(tc, hsi, msi, att1, att2, wg, bg, wp, 
             return 0 <= i < NCH
 
         def vector_share(i):
-            return CH if i < 2 else VS
+            return CH if i < 2 else 256 if i == NCH - 1 else VS
 
         def on_tensor(i):
             return TPE + 1 if i >= NCH - EXTRA else TPE
@@ -367,16 +367,22 @@ def tile_crossattentionfusion_pa_t_kernel(tc, hsi, msi, att1, att2, wg, bg, wp, 
             products(i)
             if i == 0:
                 stage1(i + 1)
-            diff_on_tensor(i + 1)
+            if i != 1:
+                diff_on_tensor(i + 1)
             regroup_first(i + 2)
             finish_first(i - 1)
             if i > 0:
                 quantise_x(i + 1)
                 stage1(i + 1)
+            if i == 1:
+                diff_on_tensor(i + 1)
             regroup_vector(i + 2)
-            regroup_second(i + 2)
+            if i + 2 < NCH - 1:
+                regroup_second(i + 2)
             finish_second(i - 1)
             sigmoid(i + 1)
+            if i + 2 == NCH - 1:
+                regroup_second(i + 2)
             diff_late(i + 1)
             fuse(i)
             if i % PER_B == PER_B - 1 and i // PER_B + 2 < B:

@@ -312,7 +312,6 @@ def tile_crossattentionfusion_pa_t_kernel(tc, hsi, msi, att1, att2, wg, bg, wp, 
         bg_raw = const.tile([P, T], BF16)
         bp_raw = const.tile([P, T], BF16)
         nc.scalar.dma_start(out=bg_raw[:], in_=bg.rearrange("(p t) -> p t", t=T))
-        nc.scalar.dma_start(out=bp_raw[:], in_=bp.rearrange("(p t) -> p t", t=T))
         wg_raw = const.tile([P, T * 2 * C], BF16)
         wp_raw = const.tile([P, T * C], BF16)
         wg_rows = wg.rearrange("(m t) k -> m (t k)", t=T)
@@ -327,6 +326,7 @@ def tile_crossattentionfusion_pa_t_kernel(tc, hsi, msi, att1, att2, wg, bg, wp, 
         load("msi", 1, 0, NPIX)
         load("a1", 0, CH, NPIX)
         load("a2", 0, CH, NPIX)
+        nc.sync.dma_start(out=bp_raw[:], in_=bp.rearrange("(p t) -> p t", t=T))
         load("a1", 1, 0, NPIX)
         load("a2", 1, 0, NPIX)
 
@@ -350,7 +350,6 @@ def tile_crossattentionfusion_pa_t_kernel(tc, hsi, msi, att1, att2, wg, bg, wp, 
         regroup_part(1, nc.scalar.copy, 0, "hsi", 0, 512)
         regroup_part(0, nc.vector.tensor_copy, 1, "msi", 0, CH)
         nc.vector.tensor_copy(out=bgf[:], in_=bg_raw[:])
-        nc.vector.tensor_copy(out=bpf[:], in_=bp_raw[:])
         quantise_x(0)
         regroup_part(1, nc.vector.tensor_copy, 1, "msi", 0, CH)
         load("hsi", 2, 0, NPIX)
@@ -389,4 +388,6 @@ def tile_crossattentionfusion_pa_t_kernel(tc, hsi, msi, att1, att2, wg, bg, wp, 
                 load("a1", i // PER_B + 2, 0, NPIX)
                 load("a2", i // PER_B + 2, 0, NPIX)
             diff_on_vector(i + 1, on_tensor(i + 1), T)
+            if i == 0:
+                nc.vector.tensor_copy(out=bpf[:], in_=bp_raw[:])
             quantise_f(i)

from contextlib import ExitStack

import concourse.mybir as mybir
from concourse.masks import make_identity

F32 = mybir.dt.float32
BF16 = mybir.dt.bfloat16
U32 = mybir.dt.uint32
U8 = mybir.dt.uint8
FP8X4 = mybir.dt.float8_e4m3fn_x4
ACT = mybir.ActivationFunctionType
ALU = mybir.AluOpType

P = 128
B = 4
C = 512
NPIX = 1024
T = 4
CH = 512
PER_B = NPIX // CH
NCH = B * PER_B
VS = 368
TPE = 2
GP = 3
ORDER = (3, 0, 1, 2)
EXTRA = 3

FLOPS = 2 * B * NPIX * (2 * C * C + C * C)


def tile_crossattentionfusion_pa_t_kernel(tc, hsi, msi, att1, att2, wg, bg, wp, bp, out):
    nc = tc.nc
    sources = {"hsi": hsi, "msi": msi, "a1": att1, "a2": att2}
    with ExitStack() as ctx:
        ctx.enter_context(tc.manual_schedule())
        const = ctx.enter_context(tc.tile_pool(name="const", bufs=1))
        xin = ctx.enter_context(tc.tile_pool(name="xin", bufs=2))
        work = ctx.enter_context(tc.tile_pool(name="work", bufs=2))
        psum = ctx.enter_context(tc.psum_pool(name="psum", bufs=2))

        raw, xg, xc, xs, gate, mix, dps = {}, {}, {}, {}, {}, {}, {}
        acc1, acc2, fc, fs, fg, y = {}, {}, {}, {}, {}, {}
        halved = set()

        def live(i):
            return 0 <= i < NCH

        def vector_share(i):
            return CH if i < 2 else 256 if i == NCH - 1 else VS

        def on_tensor(i):
            return TPE + 1 if i >= NCH - EXTRA else TPE

        def load(name, b, lo, hi):
            if (name, b) not in raw:
                raw[(name, b)] = xin.tile([P, T * NPIX], BF16, tag=name, name="%s%d" % (name, b))
            if hi - lo == NPIX:
                nc.sync.dma_start(
                    out=raw[(name, b)][:].rearrange("p (t n) -> p t n", t=T),
                    in_=sources[name][b].rearrange("(p t) h w -> p t (h w)", t=T),
                )
            else:
                halved.add((name, b))
                nc.sync.dma_start(
                    out=raw[(name, b)][:, T * lo : T * hi].rearrange("p (t n) -> p t n", t=T),
                    in_=sources[name][b].rearrange("(p t) h w -> p t (h w)", t=T)[:, :, lo:hi],
                )

        def planes(name, i):
            b, lo = i // PER_B, (i % PER_B) * CH
            if (name, b) in halved:
                return raw[(name, b)][:, T * lo : T * (lo + CH)].rearrange("p (t n) -> p t n", t=T)
            return raw[(name, b)][:].rearrange("p (t n) -> p t n", t=T)[:, :, lo : lo + CH]

        def regroup_part(i, copy, s, name, lo, hi):
            copy(
                out=xg[i][:, s, lo * T : hi * T].rearrange("p (c i j) -> p c j i", i=4, j=T),
                in_=planes(name, i)[:, :, lo:hi].rearrange("p j (c i) -> p c j i", i=4),
            )

        def regroup_open(i):
            xg[i] = work.tile([P, 2, CH * T], BF16, tag="xg", bufs=3, align_bytes=64, name="xg%d" % i)

        def regroup_first(i):
            if not live(i):
                return
            regroup_open(i)
            regroup_part(i, nc.scalar.copy, 0, "hsi", 0, CH)

        def regroup_vector(i):
            if live(i):
                regroup_part(i, nc.vector.tensor_copy, 1, "msi", 0, vector_share(i))

        def regroup_second(i):
            if not live(i):
                return
            if vector_share(i) < CH:
                regroup_part(i, nc.scalar.copy, 1, "msi", vector_share(i), CH)
            b = i // PER_B
            if i % PER_B == PER_B - 1 and b + 2 < B:
                load("hsi", b + 2, 0, NPIX)
                load("msi", b + 2, 0, NPIX)

        def quantise_x(i):
            if not live(i):
                return
            xc[i] = work.tile([P, 2, CH], U32, tag="xc", align_bytes=64, name="xc%d" % i)
            xs[i] = work.tile([P, 2, CH], U8, tag="xs", align_bytes=64, name="xs%d" % i)
            nc.vector.quantize_mx(
                out=xc[i][:].rearrange("p s w -> p (s w)").bitcast(FP8X4),
                scales=xs[i][:].rearrange("p s w -> p (s w)"),
                in_=xg[i][:].rearrange("p s w -> p (s w)"),
            )

        def diff_on_vector(i, lo, hi):
            if not live(i) or lo >= hi:
                return
            if i not in mix:
                mix[i] = work.tile([P, T, CH], F32, tag="mix", name="mix%d" % i)
            nc.vector.tensor_tensor(
                out=mix[i][:, lo:hi, :], in0=planes("a1", i)[:, lo:hi, :], in1=planes("a2", i)[:, lo:hi, :], op=ALU.subtract
            )

        def diff_plane(i, t, tag, bufs):
            dps[(i, t)] = psum.tile([P, CH], F32, tag=tag, bufs=bufs, name="dps%d_%d" % (i, t))
            nc.tensor.matmul(out=dps[(i, t)][:], lhsT=ident_b[:], rhs=planes("a1", i)[:, t, :], start=True, stop=False)
            nc.tensor.matmul(out=dps[(i, t)][:], lhsT=minus_b[:], rhs=planes("a2", i)[:, t, :], start=False, stop=True)

        def diff_on_tensor(i):
            if not live(i):
                return
            for t in range(TPE):
                diff_plane(i, t, "dps", 2)

        def diff_late(i):
            if live(i) and on_tensor(i) > TPE:
                diff_plane(i, TPE, "s1", 4)

        def stage1(i):
            if not live(i):
                return
            for t in ORDER:
                acc1[(i, t)] = psum.tile([P, CH], F32, tag="s1", bufs=4, name="s1_%d_%d" % (i, t))
                for s in range(2):
                    k = 2 * t + s
                    nc.tensor.matmul_mx(
                        out=acc1[(i, t)][:],
                        lhsT=wgc[:, k * P : (k + 1) * P].bitcast(FP8X4),
                        lhsT_scale=wgs[:, k * P : (k + 1) * P],
                        rhs=xc[i][:, s, :].bitcast(FP8X4),
                        rhs_scale=xs[i][:, s, :],
                        start=(s == 0),
                        stop=(s == 1),
                    )

        def sigmoid(i):
            if not live(i):
                return
            gate[i] = work.tile([P, T, CH], F32, tag="gate", name="gate%d" % i)
            for t in ORDER:
                nc.scalar.activation(
                    out=gate[i][:, t, :], in_=acc1[(i, t)][:], func=ACT.Sigmoid, bias=bgf[:, t : t + 1], scale=1.0
                )

        def pieces(i):
            return ((0, CH // 2), (CH // 2, CH)) if i == NCH - 1 else ((0, CH),)

        def product(i, t, a, b):
            nc.vector.tensor_tensor(out=mix[i][:, t, a:b], in0=gate[i][:, t, a:b], in1=dps[(i, t)][:, a:b], op=ALU.mult)

        def products(i):
            if not live(i):
                return
            lo = on_tensor(i)
            nc.gpsimd.tensor_tensor(out=mix[i][:, GP, :], in0=gate[i][:, GP, :], in1=mix[i][:, GP, :], op=ALU.mult)
            if i == NCH - 1:
                product(i, 0, 0, CH)
                product(i, 1, 0, CH // 2)
                product(i, 2, 0, CH // 2)
                product(i, 1, CH // 2, CH)
                return
            for t in range(lo):
                product(i, t, 0, CH)
            if lo < GP:
                nc.vector.tensor_tensor(
                    out=mix[i][:, lo:GP, :], in0=gate[i][:, lo:GP, :], in1=mix[i][:, lo:GP, :], op=ALU.mult
                )

        def fuse_piece(i, a, b):
                nc.vector.tensor_tensor(
                    out=fg[i][:, a * T : b * T].rearrange("p (c i t) -> p c t i", i=8, t=T),
                    in0=mix[i][:, :, a:b].rearrange("p t (c i) -> p c t i", i=8),
                    in1=planes("a2", i)[:, :, a:b].rearrange("p t (c i) -> p c t i", i=8),
                    op=ALU.add,
                )

        def fuse(i):
            if not live(i):
                return
            fg[i] = work.tile([P, CH * T], BF16, tag="fg", align_bytes=64, name="fg%d" % i)
            if i == NCH - 1:
                fuse_piece(i, 0, CH // 2)
                product(i, 2, CH // 2, CH)
            else:
                fuse_piece(i, 0, CH)

        def quantise_f(i):
            if not live(i):
                return
            fc[i] = work.tile([P, CH], U32, tag="fc", align_bytes=64, name="fc%d" % i)
            fs[i] = work.tile([P, CH], U8, tag="fs", align_bytes=64, name="fs%d" % i)
            for a, b in pieces(i):
                if a > 0:
                    fuse_piece(i, a, b)
                nc.vector.quantize_mx(out=fc[i][:, a:b].bitcast(FP8X4), scales=fs[i][:, a:b], in_=fg[i][:, a * T : b * T])
                for t in range(T if i == NCH - 1 else 2):
                    stage2(i, t, a, b)

        def bank(i, t, a):
            if i < NCH - 1 or (a == 0 and t < 2):
                return "s2", 2
            if a == 0 or t < 2:
                return "s1", 4
            return "dps", 2

        def stage2(i, t, a, b):
            tag, bufs = bank(i, t, a)
            acc2[(i, t, a)] = psum.tile([P, b - a], F32, tag=tag, bufs=bufs, name="s2_%d_%d_%d" % (i, t, a))
            nc.tensor.matmul_mx(
                out=acc2[(i, t, a)][:],
                lhsT=wpc[:, t * P : (t + 1) * P].bitcast(FP8X4),
                lhsT_scale=wps[:, t * P : (t + 1) * P],
                rhs=fc[i][:, a:b].bitcast(FP8X4),
                rhs_scale=fs[i][:, a:b],
                start=True,
                stop=True,
            )

        def add_bias(i, t, a, b, on_vector):
            if on_vector:
                nc.vector.tensor_scalar_add(out=y[i][:, t, a:b], in0=acc2[(i, t, a)][:], scalar1=bpf[:, t : t + 1])
            else:
                nc.scalar.activation(
                    out=y[i][:, t, a:b], in_=acc2[(i, t, a)][:], func=ACT.Identity, bias=bpf[:, t : t + 1], scale=1.0
                )

        def store(i, t_lo, t_hi, a, b):
            lo = (i % PER_B) * CH
            nc.sync.dma_start(
                out=out[i // PER_B].rearrange("(p t) h w -> p t (h w)", t=T)[:, t_lo:t_hi, lo + a : lo + b],
                in_=y[i][:, t_lo:t_hi, a:b],
            )

        def finish_first(i):
            if not live(i):
                return
            y[i] = work.tile([P, T, CH], F32, tag="y", bufs=3, name="y%d" % i)
            if i == NCH - 1:
                return
            for t in range(2):
                add_bias(i, t, 0, CH, False)
                stage2(i, t + 2, 0, CH)
                if i == NCH - 2:
                    store(i, t, t + 1, 0, CH)
            if i < NCH - 2:
                store(i, 0, 2, 0, CH)

        def finish_second(i):
            if not live(i):
                return
            if i < NCH - 1:
                for t in range(2, T):
                    add_bias(i, t, 0, CH, False)
                    if i == NCH - 2:
                        store(i, t, t + 1, 0, CH)
                if i < NCH - 2:
                    store(i, 2, T, 0, CH)
                return
            for a, b in pieces(i):
                for t in range(T):
                    add_bias(i, t, a, b, a > 0 and t < T - 1)
                    store(i, t, t + 1, a, b)

        def transpose_weight(raw_w, passes, label, tag, bufs, copy):
            combos = T * passes
            words = raw_w[:].bitcast(F32).rearrange("m (t c p u) -> m t c p u", t=T, c=passes, p=P, u=2)
            grouped = const.tile([P, combos * P * 4], BF16, align_bytes=64, name=label + "_grouped")
            gwords = grouped[:].bitcast(F32).rearrange("p (k m u) -> p k m u", k=combos, m=P, u=2)
            for bank in range(combos // 2):
                tp = psum.tile([P, 4, P], F32, tag=tag, bufs=bufs, name="%s_tp%d" % (label, bank))
                for kk in range(2):
                    k = 2 * bank + kk
                    for u in range(2):
                        nc.tensor.transpose(
                            out=tp[:, 2 * kk + u, :], in_=words[:, k // passes, k % passes, :, u], identity=ident[:]
                        )
                copy(out=gwords[:, 2 * bank : 2 * bank + 2, :, :], in_=tp[:].rearrange("p (k u) m -> p k m u", k=2, u=2))
            return grouped

        def quantise_weight(grouped, passes, label):
            combos = T * passes
            codes = const.tile([P, combos * P], U32, align_bytes=64, name=label + "_codes")
            scales = const.tile([P, combos * P], U8, align_bytes=64, name=label + "_scales")
            for half in range(combos // 4):
                nc.vector.quantize_mx(
                    out=codes[:, half * 512 : (half + 1) * 512].bitcast(FP8X4),
                    scales=scales[:, half * 512 : (half + 1) * 512],
                    in_=grouped[:, half * 2048 : (half + 1) * 2048],
                )
            return codes, scales

        bg_raw = const.tile([P, T], BF16)
        bp_raw = const.tile([P, T], BF16)
        nc.scalar.dma_start(out=bg_raw[:], in_=bg.rearrange("(p t) -> p t", t=T))
        wg_raw = const.tile([P, T * 2 * C], BF16)
        wp_raw = const.tile([P, T * C], BF16)
        wg_rows = wg.rearrange("(m t) k -> m (t k)", t=T)
        nc.sync.dma_start(out=wg_raw[:, : T * C], in_=wg_rows[:, : T * C])
        nc.sync.dma_start(out=wg_raw[:, T * C :], in_=wg_rows[:, T * C :])
        load("hsi", 0, 0, NPIX)
        load("msi", 0, 0, NPIX)
        nc.sync.dma_start(out=wp_raw[:], in_=wp.rearrange("(m t) k -> m (t k)", t=T))
        load("a1", 0, 0, CH)
        load("a2", 0, 0, CH)
        load("hsi", 1, 0, NPIX)
        load("msi", 1, 0, NPIX)
        load("a1", 0, CH, NPIX)
        load("a2", 0, CH, NPIX)
        nc.sync.dma_start(out=bp_raw[:], in_=bp.rearrange("(p t) -> p t", t=T))
        load("a1", 1, 0, NPIX)
        load("a2", 1, 0, NPIX)

        warm = const.tile([P, 1], F32)
        nc.vector.memset(warm[:], 0.0)
        warm2 = const.tile([P, 1], F32)
        nc.scalar.activation(out=warm2[:], in_=warm[:], func=ACT.Sigmoid)
        ident = const.tile([P, P], F32)
        make_identity(nc, ident[:])
        ident_b = const.tile([P, P], BF16)
        make_identity(nc, ident_b[:])
        minus_b = const.tile([P, P], BF16)
        nc.vector.tensor_scalar_mul(out=minus_b[:], in0=ident_b[:], scalar1=-1.0)
        bgf = const.tile([P, T], F32)
        bpf = const.tile([P, T], F32)

        wg_grouped = transpose_weight(wg_raw, 2, "wg", "s1", 4, nc.scalar.copy)
        wgc, wgs = quantise_weight(wg_grouped, 2, "wg")
        regroup_first(0)
        regroup_open(1)
        regroup_part(1, nc.scalar.copy, 0, "hsi", 0, 512)
        regroup_part(0, nc.vector.tensor_copy, 1, "msi", 0, CH)
        nc.vector.tensor_copy(out=bgf[:], in_=bg_raw[:])
        quantise_x(0)
        regroup_part(1, nc.vector.tensor_copy, 1, "msi", 0, CH)
        load("hsi", 2, 0, NPIX)
        load("msi", 2, 0, NPIX)
        wp_grouped = transpose_weight(wp_raw, 1, "wp", "s2", 2, nc.scalar.copy)
        wpc, wps = quantise_weight(wp_grouped, 1, "wp")
        quantise_x(1)
        stage1(0)
        diff_on_vector(0, on_tensor(0), T)
        diff_on_tensor(0)
        sigmoid(0)

        for i in range(NCH + 1):
            products(i)
            if i == 0:
                stage1(i + 1)
            if i != 1:
                diff_on_tensor(i + 1)
            regroup_first(i + 2)
            finish_first(i - 1)
            if i > 0:
                quantise_x(i + 1)
                stage1(i + 1)
            if i == 1:
                diff_on_tensor(i + 1)
            regroup_vector(i + 2)
            if i + 2 < NCH - 1:
                regroup_second(i + 2)
            finish_second(i - 1)
            sigmoid(i + 1)
            if i + 2 == NCH - 1:
                regroup_second(i + 2)
            diff_late(i + 1)
            fuse(i)
            if i % PER_B == PER_B - 1 and i // PER_B + 2 < B:
                load("a1", i // PER_B + 2, 0, NPIX)
                load("a2", i // PER_B + 2, 0, NPIX)
            diff_on_vector(i + 1, on_tensor(i + 1), T)
            if i == 0:
                nc.vector.tensor_copy(out=bpf[:], in_=bp_raw[:])
            quantise_f(i)
